import numpy as np
import ml_dtypes


def mxq(x, axis, fmt="e4m3"):
    dtype, down = {"e4m3": (ml_dtypes.float8_e4m3fn, 7), "e5m2": (ml_dtypes.float8_e5m2, 14)}[fmt]
    v = np.moveaxis(np.asarray(x, np.float32).astype(ml_dtypes.bfloat16).astype(np.float64), axis, -1)
    blocks = v.reshape(v.shape[:-1] + (-1, 32))
    amax = np.abs(blocks).max(-1, keepdims=True)
    byte = np.maximum(np.where(amax > 0, np.frexp(amax)[1] - 1 + 127, 0) - down, 1)
    scale = np.exp2(byte - 127.0)
    codes = (blocks / scale).astype(np.float32).astype(dtype).astype(np.float64)
    return np.moveaxis((codes * scale).reshape(v.shape), -1, axis)


WIDE = False


def mx_kscale(k):
    if not WIDE:
        return np.ones(k)
    levels = np.array([10, -10, 5, -5, 0])
    if k % 512:
        return np.exp2(np.random.permutation(np.resize(levels, k // 32))).repeat(32)
    a = np.empty((k // 512, 16))
    for p in range(k // 512):
        a[p, :8] = np.random.permutation(np.resize(levels, 8))
        for g in range(8):
            far = levels[np.abs(levels - a[p, g]) >= 10]
            a[p, g + 8] = far[np.random.randint(len(far))]
    return np.exp2(a.ravel()).repeat(32)


BF16 = ml_dtypes.bfloat16


def bf(x):
    return np.asarray(x, np.float32).astype(BF16)


def f64(x):
    return np.asarray(x).astype(np.float64)


B, C, H, W = 2, 2048, 64, 64
N = H * W
KV = 0.05 * N / np.sqrt(C)


def setup_inputs():
    s, t = mx_kscale(C), mx_kscale(C)
    return {"x": bf(np.random.standard_normal((B, C, H, W)) * s[None, :, None, None]),
            "mask": bf(np.random.random_sample((B, 1, H, W))),
            "W_q": bf(np.random.standard_normal((C, C)) / np.sqrt(C) / s[:, None]),
            "b_q": bf(np.random.standard_normal(C) * 0.3),
            "kv_know": bf(np.random.standard_normal((B, 1, C)) * KV * t),
            "kv_mask": bf(np.random.standard_normal((B, 1, C)) * KV * t),
            "W_out": bf(np.random.standard_normal((C, C)) / KV / t[:, None]),
            "b_out": bf(np.random.standard_normal(C) * 0.2)}


def reference(x, mask, W_q, b_q, kv_know, kv_mask, W_out, b_out):
    x, mask = f64(x), f64(mask)
    b, c, h, w = x.shape
    xf = np.transpose(x, (0, 2, 3, 1)).reshape(b, h * w, c)
    q = (mxq(xf, 2, "e4m3") @ mxq(f64(W_q), 0, "e4m3")) + f64(b_q)
    q = q / np.linalg.norm(q, axis=-1, keepdims=True)
    m = np.transpose(mask, (0, 2, 3, 1)).reshape(b, h * w, 1)
    inv = 1.0 - m
    qu = q * inv
    qm = q * m
    out_know = f64(kv_know) * qu
    out_mask = f64(kv_mask) * qm
    out = out_know * inv + m * (0.3 * out_know + 0.7 * out_mask)
    return (mxq(out, 2, "e4m3") @ mxq(f64(W_out), 0, "e4m3")) + f64(b_out)

@@ -1,0 +1,449 @@
+from contextlib import ExitStack
+
+import concourse.mybir as mybir
+from concourse.masks import make_identity
+
+F32 = mybir.dt.float32
+BF16 = mybir.dt.bfloat16
+U32 = mybir.dt.uint32
+U8 = mybir.dt.uint8
+FP8X4 = mybir.dt.float8_e4m3fn_x4
+ACT = mybir.ActivationFunctionType
+ALU = mybir.AluOpType
+
+IMAGES = 2
+C = 2048
+PIX = 4096
+P = 128
+PACK = 4
+KPASS = P * PACK
+NPASS = C // KPASS
+T = 512
+NBLK = IMAGES * PIX // T
+BLK_PER_IMG = PIX // T
+NCT = C // P
+FLOPS = 2 * 2 * IMAGES * PIX * C * C
+
+ACC_G = ()
+LAG = 1
+DELAY = 10
+RAW_BUFS = 4
+IL_BUFS = 4
+U_BUFS = 3
+SQ_BUFS = 3
+QU_BUFS = 6
+Y_BUFS = 3
+S1_BUFS = 3
+S2_BUFS = 3
+QLAG = 1
+HEAD_PLAN = {
+    -1: "xvxsxvxsqsqvqvqsqvqvqsqv",
+    0: "xvqsqvqsqsxv",
+    1: "qvqsqvqvxv",
+    2: "osxs",
+    3: "osxv",
+    4: "ovosxv",
+    5: "ososxv",
+    6: "ososxv",
+    7: "ososxv",
+    8: "ovososxv",
+    9: "osovosxv",
+}
+
+
+def tile_hydraattention_pb_l_kernel(tc, x, mask, W_q, b_q, kv_know, kv_mask, W_out, b_out, out):
+    nc = tc.nc
+    xv = x.rearrange("b c h w -> b c (h w)")
+    mrows = mask.rearrange("b o h w -> (b o h w)").rearrange("(c p) -> c p", p=P)
+
+    with ExitStack() as ctx:
+        sb = ctx.enter_context(tc.tile_pool(name="sb", bufs=1))
+        ps = ctx.enter_context(tc.psum_pool(name="ps", bufs=1))
+        ctx.enter_context(tc.manual_schedule())
+
+        wqc = sb.tile([P, NPASS, C], U32, name="wqc", align_bytes=64)
+        wqs = sb.tile([P, C], U8, name="wqs", align_bytes=64)
+        woc = sb.tile([P, NPASS, C], U32, name="woc", align_bytes=64)
+        wos = sb.tile([P, C], U8, name="wos", align_bytes=64)
+
+        jobs = []
+        cnt = {"load": 0, "il": 0, "q": 0}
+        raws = {}
+        ils = {}
+        xcs = {}
+        xss = {}
+
+        def x_dst(i, g):
+            def dst():
+                if i not in xcs:
+                    xc_t = sb.tile([P, NPASS, T], U32, tag="xc", bufs=2, align_bytes=64, name="xc")
+                    xs_t = sb.tile([P, T], U8, tag="xs", bufs=2, align_bytes=64, name="xs")
+                    xcs[i] = xc_t
+                    xss[i] = xs_t
+                return xcs[i][:, g, :], xss[i][4 * g : P, :]
+
+            return dst
+
+        def w_dst(codes, planes, g, c0):
+            def dst():
+                return codes[:, g, c0 : c0 + KPASS], planes[4 * g : P, c0 : c0 + KPASS]
+
+            return dst
+
+        def load_more():
+            while cnt["load"] < len(jobs) and cnt["load"] < cnt["il"] + RAW_BUFS:
+                n = cnt["load"]
+                raw = sb.tile([P, PACK, KPASS], BF16, tag="raw", bufs=RAW_BUFS, name="raw")
+                nc.sync.dma_start(out=raw[:], in_=jobs[n][0].rearrange("(p j) w -> p j w", j=PACK))
+                raws[n] = raw
+                cnt["load"] = n + 1
+
+        def il_next():
+            n = cnt["il"]
+            raw = raws.pop(n)
+            il = sb.tile([P, PACK * KPASS], BF16, tag="il", bufs=IL_BUFS, align_bytes=64, name="il")
+            if jobs[n][1]:
+                dst = il[:].rearrange("p (t m j) -> p t m j", t=PACK, j=PACK)
+                src = raw[:].rearrange("p j (m t) -> p t m j", t=PACK)
+            else:
+                dst = il[:].rearrange("p (w j) -> p w j", j=PACK)
+                src = raw[:].rearrange("p j w -> p w j")
+            if jobs[n][2] == "v":
+                nc.vector.tensor_copy(out=dst, in_=src)
+            elif jobs[n][2] == "g":
+                nc.gpsimd.tensor_scalar(out=dst, in0=src, scalar1=1.0, scalar2=0.0, op0=ALU.mult, op1=ALU.add)
+            else:
+                nc.scalar.copy(out=dst, in_=src)
+            ils[n] = il
+            cnt["il"] = n + 1
+            load_more()
+
+        def q_next():
+            n = cnt["q"]
+            il = ils.pop(n)
+            codes, plane = jobs[n][3]()
+            nc.vector.quantize_mx(out=codes.bitcast(FP8X4), scales=plane, in_=il[:])
+            cnt["q"] = n + 1
+
+        def need(key):
+            while cnt["q"] <= last_job[key]:
+                if cnt["il"] <= cnt["q"]:
+                    il_next()
+                q_next()
+
+        def il_step():
+            il_next()
+            while cnt["q"] < cnt["il"] - QLAG:
+                q_next()
+
+        NA = NBLK * NPASS
+        head_plan = HEAD_PLAN
+        x_list = [(i, g) for i in range(NBLK) for g in range(NPASS)]
+        q_list = [(grp, g) for grp in range(NPASS) for g in range(NPASS)]
+        o_list = [(n, g) for n in range(NPASS) for g in range(NPASS)]
+        last_job = {}
+
+        def add_job(kind, eng):
+            if kind == "x":
+                i, g = x_list.pop(0)
+                b = i // BLK_PER_IMG
+                t0 = (i % BLK_PER_IMG) * T
+                jobs.append((xv[b, g * KPASS : (g + 1) * KPASS, t0 : t0 + T], False, eng, x_dst(i, g)))
+                last_job[("x", i)] = len(jobs) - 1
+            elif kind == "q":
+                grp, g = q_list.pop(0)
+                src = W_q[g * KPASS : (g + 1) * KPASS, grp * KPASS : (grp + 1) * KPASS]
+                jobs.append((src, True, eng, w_dst(wqc, wqs, g, grp * KPASS)))
+                last_job[("q", grp)] = len(jobs) - 1
+            else:
+                n, g = o_list.pop(0)
+                src = W_out[g * KPASS : (g + 1) * KPASS, n * KPASS : (n + 1) * KPASS]
+                jobs.append((src, False, eng, w_dst(woc, wos, g, n * KPASS)))
+                last_job[("o", n)] = len(jobs) - 1
+
+        n_prep = {}
+        for n in range(-1, NA):
+            if n in head_plan:
+                for r in range(len(head_plan[n]) // 2):
+                    add_job(head_plan[n][2 * r], head_plan[n][2 * r + 1])
+                n_prep[n] = len(head_plan[n]) // 2
+            elif x_list:
+                add_job("x", "s")
+                n_prep[n] = 1
+
+        load_more()
+
+        mrow = sb.tile([P, P], BF16, name="mrow")
+        nc.vector.memset(mrow[:], 0.0)
+        nc.scalar.dma_start(out=mrow[0:64, :], in_=mrows)
+        bq_r = sb.tile([P, NPASS, PACK], BF16, name="bq_r")
+        nc.scalar.dma_start(out=bq_r[:], in_=b_q.rearrange("(g p j) -> p g j", p=P, j=PACK))
+        kk_r = sb.tile([P, IMAGES * NPASS, PACK], BF16, name="kk_r")
+        nc.scalar.dma_start(out=kk_r[:], in_=kv_know.rearrange("b o (g p j) -> p (b o g) j", p=P, j=PACK))
+        km_r = sb.tile([P, IMAGES * NPASS, PACK], BF16, name="km_r")
+        nc.scalar.dma_start(out=km_r[:], in_=kv_mask.rearrange("b o (g p j) -> p (b o g) j", p=P, j=PACK))
+        bob = sb.tile([P, C], BF16, name="bob")
+        nc.scalar.dma_start(out=bob[:], in_=b_out.partition_broadcast(P))
+
+        warm = sb.tile([P, 1], F32, name="warm")
+        nc.vector.memset(warm[:], 1.0)
+        warm2 = sb.tile([P, 1], F32, name="warm2")
+        nc.scalar.activation(out=warm2[:], in_=warm[:], func=ACT.Sqrt)
+
+        ones2 = sb.tile([P, 2], F32, name="ones2")
+        nc.vector.memset(ones2[:], 1.0)
+        identb = sb.tile([P, P], BF16, name="identb")
+        make_identity(nc, identb[:])
+        identf = sb.tile([P, P], F32, name="identf")
+        make_identity(nc, identf[:])
+
+        def const_math():
+            bq = sb.tile([P, NCT], F32, name="bq")
+            nc.vector.tensor_copy(out=bq[:], in_=bq_r[:].rearrange("p g j -> p (g j)"))
+            kvk = sb.tile([P, IMAGES * NCT], F32, name="kvk")
+            nc.vector.tensor_copy(out=kvk[:], in_=kk_r[:].rearrange("p g j -> p (g j)"))
+            dk = sb.tile([P, IMAGES * NCT], F32, name="dk")
+            nc.vector.tensor_tensor(
+                out=dk[:],
+                in0=km_r[:].rearrange("p g j -> p (g j)"),
+                in1=kk_r[:].rearrange("p g j -> p (g j)"),
+                op=ALU.subtract,
+            )
+            m_ps = ps.tile([P, P], BF16, tag="misc", bufs=1, name="m_ps")
+            nc.tensor.transpose(out=m_ps[:], in_=mrow[:], identity=identb[:])
+            nchunk = IMAGES * PIX // P
+            mc = sb.tile([P, nchunk], F32, name="mc")
+            nc.vector.tensor_copy(out=mc[:], in_=m_ps[:, 0:nchunk])
+            inv = sb.tile([P, nchunk], F32, name="inv")
+            nc.vector.tensor_scalar(out=inv[:], in0=mc[:], scalar1=-1.0, scalar2=1.0, op0=ALU.mult, op1=ALU.add)
+            e07 = sb.tile([P, nchunk], F32, name="e07")
+            nc.vector.tensor_scalar(out=e07[:], in0=mc[:], scalar1=-0.7, scalar2=1.0, op0=ALU.mult, op1=ALU.add)
+            ca = sb.tile([P, nchunk], F32, name="ca")
+            nc.vector.tensor_tensor(out=ca[:], in0=inv[:], in1=e07[:], op=ALU.mult)
+            cb = sb.tile([P, nchunk], F32, name="cb")
+            nc.vector.scalar_tensor_tensor(out=cb[:], in0=mc[:], scalar=0.7, in1=mc[:], op0=ALU.mult, op1=ALU.mult)
+            sig = sb.tile([P, nchunk], F32, name="sig")
+            nc.vector.tensor_tensor(out=sig[:], in0=ca[:], in1=cb[:], op=ALU.add)
+            rsig = sb.tile([P, nchunk], F32, name="rsig")
+            nc.vector.reciprocal(out=rsig[:], in_=sig[:])
+            wc = sb.tile([P, nchunk], F32, name="wc")
+            nc.vector.tensor_tensor(out=wc[:], in0=cb[:], in1=rsig[:], op=ALU.mult)
+            return bq, kvk, dk, sig, wc
+
+        wbs = {}
+        us = {}
+        qus = {}
+        accs = {}
+        npss = {}
+        scs = {}
+        spss = {}
+        gis = {}
+        gcs = {}
+        gss = {}
+        ys = {}
+
+        def w_bcast(i):
+            wps = ps.tile([P, T], F32, tag="misc", bufs=1, name="wps")
+            for k in range(T // P):
+                col = i * (T // P) + k
+                nc.tensor.matmul(
+                    out=wps[:, k * P : (k + 1) * P],
+                    lhsT=wc[:, col : col + 1].to_broadcast([P, P]),
+                    rhs=identf[:],
+                    start=True,
+                    stop=True,
+                )
+            wb = sb.tile([P, T], F32, tag="wb", bufs=2, name="wb")
+            nc.scalar.copy(out=wb[:], in_=wps[:])
+            wbs[i] = wb
+
+        def u_tile(n):
+            if n in us or n >= NBLK * NCT:
+                return
+            i = n // NCT
+            col = (i // BLK_PER_IMG) * NCT + n % NCT
+            u = sb.tile([P, T], F32, tag="u", bufs=U_BUFS, name="u")
+            nc.scalar.activation(
+                out=u[:], in_=wbs[i][:], func=ACT.Identity, bias=kvk[:, col : col + 1], scale=dk[:, col : col + 1]
+            )
+            us[n] = u
+
+        def a_tile(i, ct):
+            n = i * NCT + ct
+            grp = ct // PACK
+            j = ct % PACK
+            need(("x", i))
+            need(("q", grp))
+            u_tile(n)
+            acc_ps = ps.tile([P, T], F32, tag="s1", bufs=S1_BUFS, name="s1")
+            for g in range(NPASS):
+                nc.tensor.matmul_mx(
+                    out=acc_ps[:],
+                    lhsT=wqc[:, g, ct * P : (ct + 1) * P].bitcast(FP8X4),
+                    lhsT_scale=wqs[4 * g : P, ct * P : (ct + 1) * P],
+                    rhs=xcs[i][:, g, :].bitcast(FP8X4),
+                    rhs_scale=xss[i][4 * g : P, :],
+                    start=(g == 0),
+                    stop=(g == NPASS - 1),
+                )
+            u_tile(n + 1)
+            eng = "g" if ct in ACC_G else "v"
+            first = (i, eng) not in accs
+            if first:
+                sq = sb.tile([P, T], F32, tag="acc%s" % eng, bufs=2, name="acc%s" % eng)
+                accs[(i, eng)] = sq
+            else:
+                sq = sb.tile([P, T], F32, tag="sq", bufs=SQ_BUFS, name="sq")
+            nc.scalar.activation(out=sq[:], in_=acc_ps[:], func=ACT.Square, bias=bq[:, ct : ct + 1], scale=1.0)
+            if j == 0:
+                qu_t = sb.tile([P, PACK, T], F32, tag="qu", bufs=QU_BUFS, name="qu")
+                qus[(i, grp)] = qu_t
+            nc.vector.scalar_tensor_tensor(
+                out=qus[(i, grp)][:, j, :],
+                in0=acc_ps[:],
+                scalar=bq[:, ct : ct + 1],
+                in1=us.pop(n)[:],
+                op0=ALU.add,
+                op1=ALU.mult,
+            )
+            if not first:
+                a = accs[(i, eng)]
+                if eng == "g":
+                    nc.gpsimd.tensor_tensor(out=a[:], in0=a[:], in1=sq[:], op=ALU.add)
+                else:
+                    nc.vector.tensor_tensor(out=a[:], in0=a[:], in1=sq[:], op=ALU.add)
+
+        def norm_pe(i):
+            nps = ps.tile([P, 2 * (T // P)], F32, tag="misc", bufs=1, name="nps")
+            parts = [accs.pop((i, e)) for e in ("v", "g") if (i, e) in accs]
+            for k in range(T // P):
+                for r in range(len(parts)):
+                    nc.tensor.matmul(
+                        out=nps[:, 2 * k : 2 * k + 2],
+                        lhsT=parts[r][:, k * P : (k + 1) * P],
+                        rhs=ones2[:],
+                        start=(r == 0),
+                        stop=(r == len(parts) - 1),
+                    )
+            nrm = sb.tile([P, T // P], F32, tag="nrm", bufs=2, name="nrm")
+            nc.scalar.activation(out=nrm[:], in_=nps[:].rearrange("p (k two) -> p k two", two=2)[:, :, 0], func=ACT.Sqrt)
+            npss[i] = nrm
+
+        def norm_small(i):
+            nrm = npss.pop(i)
+            rn = sb.tile([P, T // P], F32, tag="rn", bufs=2, name="rn")
+            nc.vector.reciprocal(out=rn[:], in_=nrm[:])
+            sc = sb.tile([P, T // P], F32, tag="sc", bufs=2, name="sc")
+            c0 = i * (T // P)
+            nc.vector.tensor_tensor(out=sc[:], in0=rn[:], in1=sig[:, c0 : c0 + T // P], op=ALU.mult)
+            scs[i] = sc
+
+        def s_bcast(i):
+            sc = scs.pop(i)
+            sps = ps.tile([P, T], F32, tag="sps", bufs=1, name="sps")
+            for k in range(T // P):
+                nc.tensor.matmul(
+                    out=sps[:, k * P : (k + 1) * P],
+                    lhsT=sc[:, k : k + 1].to_broadcast([P, P]),
+                    rhs=identf[:],
+                    start=True,
+                    stop=True,
+                )
+            spss[i] = sps
+
+        def g_op(i, grp):
+            gi = sb.tile([P, T, PACK], BF16, tag="gi", bufs=2, align_bytes=64, name="gi")
+            nc.vector.tensor_tensor(
+                out=gi[:],
+                in0=qus.pop((i, grp))[:].rearrange("p j t -> p t j"),
+                in1=spss[i][:].unsqueeze(2).to_broadcast([P, T, PACK]),
+                op=ALU.mult,
+            )
+            gis[(i, grp)] = gi
+
+        def g_q(i, grp):
+            if i not in gcs:
+                gc_t = sb.tile([P, NPASS, T], U32, tag="gc", bufs=LAG + 1, align_bytes=64, name="gc")
+                gs_t = sb.tile([P, T], U8, tag="gs", bufs=LAG + 1, align_bytes=64, name="gs")
+                gcs[i] = gc_t
+                gss[i] = gs_t
+            nc.vector.quantize_mx(
+                out=gcs[i][:, grp, :].bitcast(FP8X4),
+                scales=gss[i][4 * grp : P, :],
+                in_=gis.pop((i, grp))[:].rearrange("p t j -> p (t j)"),
+            )
+
+        def b_bank(k, tt, n):
+            b = k // BLK_PER_IMG
+            row0 = (k % BLK_PER_IMG) * T + tt * P
+            need(("o", n))
+            y_ps = ps.tile([P, KPASS], F32, tag="s2", bufs=S2_BUFS, name="s2")
+            for g in range(NPASS):
+                nc.tensor.matmul_mx(
+                    out=y_ps[:],
+                    lhsT=gcs[k][:, g, tt * P : (tt + 1) * P].bitcast(FP8X4),
+                    lhsT_scale=gss[k][4 * g : P, tt * P : (tt + 1) * P],
+                    rhs=woc[:, g, n * KPASS : (n + 1) * KPASS].bitcast(FP8X4),
+                    rhs_scale=wos[4 * g : P, n * KPASS : (n + 1) * KPASS],
+                    start=(g == 0),
+                    stop=(g == NPASS - 1),
+                )
+            half = n % 2
+            if half == 0:
+                y_t = sb.tile([P, 2 * KPASS], F32, tag="y", bufs=Y_BUFS, name="y")
+                ys[0] = y_t
+            nc.vector.tensor_tensor(
+                out=ys[0][:, half * KPASS : (half + 1) * KPASS],
+                in0=y_ps[:],
+                in1=bob[:, n * KPASS : (n + 1) * KPASS],
+                op=ALU.add,
+            )
+            if half == 1:
+                nc.sync.dma_start(out=out[b, row0 : row0 + P, (n - 1) * KPASS : (n + 1) * KPASS], in_=ys[0][:])
+
+        g_ready = []
+
+        def prep_steps(k):
+            return [il_step for r in range(k)]
+
+        def spread(steps, pos, npos):
+            lo = len(steps) * pos // npos
+            hi = len(steps) * (pos + 1) // npos
+            for f in steps[lo:hi]:
+                f()
+
+        def pair(n):
+            steps = prep_steps(n_prep.get(n, 0))
+            gt = g_ready.pop(0) if g_ready else None
+            if steps:
+                steps.pop(0)()
+            if gt is not None:
+                g_op(gt[0], gt[1])
+            for j in range(PACK):
+                if n < NA:
+                    a_tile(n // NPASS, (n % NPASS) * PACK + j)
+                if n >= DELAY:
+                    b_bank((n - DELAY) // 4, (n - DELAY) % 4, j)
+                spread(steps, j, PACK)
+                if j == 1 and gt is not None:
+                    g_q(gt[0], gt[1])
+            if n % NPASS == 1 and n // NPASS + 1 < NBLK and n > 1:
+                w_bcast(n // NPASS + 1)
+            if n % NPASS == 0 and NPASS <= n <= NA:
+                norm_pe(n // NPASS - 1)
+                norm_small(n // NPASS - 1)
+            if n % NPASS == 1 and NPASS <= n <= NA + 1:
+                i = n // NPASS - 1
+                s_bcast(i)
+                for grp in range(NPASS):
+                    g_ready.append((i, grp))
+
+        steps = prep_steps(n_prep[-1])
+        spread(steps, 0, 3)
+        bq, kvk, dk, sig, wc = const_math()
+        spread(steps, 1, 3)
+        w_bcast(0)
+        spread(steps, 2, 3)
+        w_bcast(1)
+        for n in range(NA + DELAY):
+            pair(n)

@@ -24,7 +24,7 @@ BLK_PER_IMG = PIX // T
 NCT = C // P
 FLOPS = 2 * 2 * IMAGES * PIX * C * C
 
-ACC_G = ()
+ACC_G = tuple(range(16))
 LAG = 1
 DELAY = 10
 RAW_BUFS = 4
@@ -36,6 +36,9 @@ Y_BUFS = 3
 S1_BUFS = 3
 S2_BUFS = 3
 QLAG = 1
+NMAJOR = False
+U_HEAD = ""
+ACC_HEAD = ""
 HEAD_PLAN = {
     -1: "xvxsxvxsqsqvqvqsqvqvqsqv",
     0: "xvqsqvqsqsxv",
@@ -54,6 +57,7 @@ HEAD_PLAN = {
 def tile_hydraattention_pb_l_kernel(tc, x, mask, W_q, b_q, kv_know, kv_mask, W_out, b_out, out):
     nc = tc.nc
     xv = x.rearrange("b c h w -> b c (h w)")
+    park = out[IMAGES - 1, PIX - IMAGES * PIX // C : PIX, :]
     mrows = mask.rearrange("b o h w -> (b o h w)").rearrange("(c p) -> c p", p=P)
 
     with ExitStack() as ctx:
@@ -192,8 +196,6 @@ def tile_hydraattention_pb_l_kernel(tc, x, mask, W_q, b_q, kv_know, kv_mask, W_o
 
         ones2 = sb.tile([P, 2], F32, name="ones2")
         nc.vector.memset(ones2[:], 1.0)
-        identb = sb.tile([P, P], BF16, name="identb")
-        make_identity(nc, identb[:])
         identf = sb.tile([P, P], F32, name="identf")
         make_identity(nc, identf[:])
 
@@ -209,26 +211,29 @@ def tile_hydraattention_pb_l_kernel(tc, x, mask, W_q, b_q, kv_know, kv_mask, W_o
                 in1=kk_r[:].rearrange("p g j -> p (g j)"),
                 op=ALU.subtract,
             )
-            m_ps = ps.tile([P, P], BF16, tag="misc", bufs=1, name="m_ps")
-            nc.tensor.transpose(out=m_ps[:], in_=mrow[:], identity=identb[:])
-            nchunk = IMAGES * PIX // P
-            mc = sb.tile([P, nchunk], F32, name="mc")
-            nc.vector.tensor_copy(out=mc[:], in_=m_ps[:, 0:nchunk])
-            inv = sb.tile([P, nchunk], F32, name="inv")
+            mc = sb.tile([P, P], F32, name="mc")
+            nc.vector.tensor_copy(out=mc[:], in_=mrow[:])
+            inv = sb.tile([P, P], F32, name="inv")
             nc.vector.tensor_scalar(out=inv[:], in0=mc[:], scalar1=-1.0, scalar2=1.0, op0=ALU.mult, op1=ALU.add)
-            e07 = sb.tile([P, nchunk], F32, name="e07")
+            e07 = sb.tile([P, P], F32, name="e07")
             nc.vector.tensor_scalar(out=e07[:], in0=mc[:], scalar1=-0.7, scalar2=1.0, op0=ALU.mult, op1=ALU.add)
-            ca = sb.tile([P, nchunk], F32, name="ca")
+            ca = sb.tile([P, P], F32, name="ca")
             nc.vector.tensor_tensor(out=ca[:], in0=inv[:], in1=e07[:], op=ALU.mult)
-            cb = sb.tile([P, nchunk], F32, name="cb")
+            cb = sb.tile([P, P], F32, name="cb")
             nc.vector.scalar_tensor_tensor(out=cb[:], in0=mc[:], scalar=0.7, in1=mc[:], op0=ALU.mult, op1=ALU.mult)
+            sig_r = sb.tile([P, P], F32, name="sig_r")
+            nc.vector.tensor_tensor(out=sig_r[:], in0=ca[:], in1=cb[:], op=ALU.add)
+            rsig = sb.tile([P, P], F32, name="rsig")
+            nc.vector.reciprocal(out=rsig[:], in_=sig_r[:])
+            w_r = sb.tile([P, P], F32, name="w_r")
+            nc.vector.tensor_tensor(out=w_r[:], in0=cb[:], in1=rsig[:], op=ALU.mult)
+            nchunk = IMAGES * PIX // P
+            nc.sync.dma_start(out=park.rearrange("r (c p) -> (r c) p", p=P), in_=w_r[0:nchunk, :])
+            s_ps = ps.tile([P, P], F32, tag="misc", bufs=1, name="s_ps")
+            nc.tensor.transpose(out=s_ps[:], in_=sig_r[:], identity=identf[:])
             sig = sb.tile([P, nchunk], F32, name="sig")
-            nc.vector.tensor_tensor(out=sig[:], in0=ca[:], in1=cb[:], op=ALU.add)
-            rsig = sb.tile([P, nchunk], F32, name="rsig")
-            nc.vector.reciprocal(out=rsig[:], in_=sig[:])
-            wc = sb.tile([P, nchunk], F32, name="wc")
-            nc.vector.tensor_tensor(out=wc[:], in0=cb[:], in1=rsig[:], op=ALU.mult)
-            return bq, kvk, dk, sig, wc
+            nc.vector.tensor_copy(out=sig[:], in_=s_ps[:, 0:nchunk])
+            return bq, kvk, dk, sig
 
         wbs = {}
         us = {}
@@ -243,18 +248,10 @@ def tile_hydraattention_pb_l_kernel(tc, x, mask, W_q, b_q, kv_know, kv_mask, W_o
         ys = {}
 
         def w_bcast(i):
-            wps = ps.tile([P, T], F32, tag="misc", bufs=1, name="wps")
-            for k in range(T // P):
-                col = i * (T // P) + k
-                nc.tensor.matmul(
-                    out=wps[:, k * P : (k + 1) * P],
-                    lhsT=wc[:, col : col + 1].to_broadcast([P, P]),
-                    rhs=identf[:],
-                    start=True,
-                    stop=True,
-                )
             wb = sb.tile([P, T], F32, tag="wb", bufs=2, name="wb")
-            nc.scalar.copy(out=wb[:], in_=wps[:])
+            per_row = C // T
+            src = park[i // per_row, (i % per_row) * T : (i % per_row + 1) * T]
+            nc.sync.dma_start(out=wb[:], in_=src.partition_broadcast(P))
             wbs[i] = wb
 
         def u_tile(n):
@@ -263,9 +260,29 @@ def tile_hydraattention_pb_l_kernel(tc, x, mask, W_q, b_q, kv_know, kv_mask, W_o
             i = n // NCT
             col = (i // BLK_PER_IMG) * NCT + n % NCT
             u = sb.tile([P, T], F32, tag="u", bufs=U_BUFS, name="u")
-            nc.scalar.activation(
-                out=u[:], in_=wbs[i][:], func=ACT.Identity, bias=kvk[:, col : col + 1], scale=dk[:, col : col + 1]
-            )
+            ue = U_HEAD[n // PACK] if n // PACK < len(U_HEAD) else "s"
+            if ue == "g":
+                nc.gpsimd.tensor_scalar(
+                    out=u[:],
+                    in0=wbs[i][:],
+                    scalar1=dk[:, col : col + 1],
+                    scalar2=kvk[:, col : col + 1],
+                    op0=ALU.mult,
+                    op1=ALU.add,
+                )
+            elif ue == "v":
+                nc.vector.tensor_scalar(
+                    out=u[:],
+                    in0=wbs[i][:],
+                    scalar1=dk[:, col : col + 1],
+                    scalar2=kvk[:, col : col + 1],
+                    op0=ALU.mult,
+                    op1=ALU.add,
+                )
+            else:
+                nc.scalar.activation(
+                    out=u[:], in_=wbs[i][:], func=ACT.Identity, bias=kvk[:, col : col + 1], scale=dk[:, col : col + 1]
+                )
             us[n] = u
 
         def a_tile(i, ct):
@@ -288,6 +305,8 @@ def tile_hydraattention_pb_l_kernel(tc, x, mask, W_q, b_q, kv_know, kv_mask, W_o
                 )
             u_tile(n + 1)
             eng = "g" if ct in ACC_G else "v"
+            if n // PACK < len(ACC_HEAD):
+                eng = ACC_HEAD[n // PACK]
             first = (i, eng) not in accs
             if first:
                 sq = sb.tile([P, T], F32, tag="acc%s" % eng, bufs=2, name="acc%s" % eng)
@@ -388,6 +407,11 @@ def tile_hydraattention_pb_l_kernel(tc, x, mask, W_q, b_q, kv_know, kv_mask, W_o
                     start=(g == 0),
                     stop=(g == NPASS - 1),
                 )
+            if NMAJOR:
+                y_t = sb.tile([P, KPASS], F32, tag="y", bufs=Y_BUFS, name="y")
+                nc.vector.tensor_tensor(out=y_t[:], in0=y_ps[:], in1=bob[:, n * KPASS : (n + 1) * KPASS], op=ALU.add)
+                nc.sync.dma_start(out=out[b, row0 : row0 + P, n * KPASS : (n + 1) * KPASS], in_=y_t[:])
+                return
             half = n % 2
             if half == 0:
                 y_t = sb.tile([P, 2 * KPASS], F32, tag="y", bufs=Y_BUFS, name="y")
@@ -423,7 +447,10 @@ def tile_hydraattention_pb_l_kernel(tc, x, mask, W_q, b_q, kv_know, kv_mask, W_o
                 if n < NA:
                     a_tile(n // NPASS, (n % NPASS) * PACK + j)
                 if n >= DELAY:
-                    b_bank((n - DELAY) // 4, (n - DELAY) % 4, j)
+                    if NMAJOR:
+                        b_bank((n - DELAY) // 4, j, (n - DELAY) % 4)
+                    else:
+                        b_bank((n - DELAY) // 4, (n - DELAY) % 4, j)
                 spread(steps, j, PACK)
                 if j == 1 and gt is not None:
                     g_q(gt[0], gt[1])
@@ -440,7 +467,7 @@ def tile_hydraattention_pb_l_kernel(tc, x, mask, W_q, b_q, kv_know, kv_mask, W_o
 
         steps = prep_steps(n_prep[-1])
         spread(steps, 0, 3)
-        bq, kvk, dk, sig, wc = const_math()
+        bq, kvk, dk, sig = const_math()
         spread(steps, 1, 3)
         w_bcast(0)
         spread(steps, 2, 3)

@@ -36,21 +36,22 @@ Y_BUFS = 3
 S1_BUFS = 3
 S2_BUFS = 3
 QLAG = 1
+Y_SG = ()
 NMAJOR = False
 U_HEAD = ""
 ACC_HEAD = ""
 HEAD_PLAN = {
-    -1: "xvxsxvxsqsqvqvqsqvqvqsqv",
-    0: "xvqsqvqsqsxv",
-    1: "qvqsqvqvxv",
-    2: "osxs",
+    -1: "xvxvxvxvqsqvqsqvqsqvqsqv",
+    0: "xvqsqvqsqvxv",
+    1: "qsqvqsqvxv",
+    2: "osxv",
     3: "osxv",
-    4: "ovosxv",
+    4: "ososxv",
     5: "ososxv",
     6: "ososxv",
     7: "ososxv",
-    8: "ovososxv",
-    9: "osovosxv",
+    8: "osososxv",
+    9: "osososxv",
 }
 
 
@@ -187,7 +188,6 @@ def tile_hydraattention_pb_l_kernel(tc, x, mask, W_q, b_q, kv_know, kv_mask, W_o
         km_r = sb.tile([P, IMAGES * NPASS, PACK], BF16, name="km_r")
         nc.scalar.dma_start(out=km_r[:], in_=kv_mask.rearrange("b o (g p j) -> p (b o g) j", p=P, j=PACK))
         bob = sb.tile([P, C], BF16, name="bob")
-        nc.scalar.dma_start(out=bob[:], in_=b_out.partition_broadcast(P))
 
         warm = sb.tile([P, 1], F32, name="warm")
         nc.vector.memset(warm[:], 1.0)
@@ -196,6 +196,8 @@ def tile_hydraattention_pb_l_kernel(tc, x, mask, W_q, b_q, kv_know, kv_mask, W_o
 
         ones2 = sb.tile([P, 2], F32, name="ones2")
         nc.vector.memset(ones2[:], 1.0)
+        identb = sb.tile([P, P], BF16, name="identb")
+        make_identity(nc, identb[:])
         identf = sb.tile([P, P], F32, name="identf")
         make_identity(nc, identf[:])
 
@@ -355,19 +357,24 @@ def tile_hydraattention_pb_l_kernel(tc, x, mask, W_q, b_q, kv_know, kv_mask, W_o
             sc = sb.tile([P, T // P], F32, tag="sc", bufs=2, name="sc")
             c0 = i * (T // P)
             nc.vector.tensor_tensor(out=sc[:], in0=rn[:], in1=sig[:, c0 : c0 + T // P], op=ALU.mult)
-            scs[i] = sc
+            s_hi = sb.tile([P, T // P], BF16, tag="s_hi", bufs=2, name="s_hi")
+            nc.vector.tensor_copy(out=s_hi[:], in_=sc[:])
+            s_lo = sb.tile([P, T // P], BF16, tag="s_lo", bufs=2, name="s_lo")
+            nc.vector.tensor_tensor(out=s_lo[:], in0=sc[:], in1=s_hi[:], op=ALU.subtract)
+            scs[i] = (s_hi, s_lo)
 
         def s_bcast(i):
             sc = scs.pop(i)
             sps = ps.tile([P, T], F32, tag="sps", bufs=1, name="sps")
             for k in range(T // P):
-                nc.tensor.matmul(
-                    out=sps[:, k * P : (k + 1) * P],
-                    lhsT=sc[:, k : k + 1].to_broadcast([P, P]),
-                    rhs=identf[:],
-                    start=True,
-                    stop=True,
-                )
+                for r in range(2):
+                    nc.tensor.matmul(
+                        out=sps[:, k * P : (k + 1) * P],
+                        lhsT=sc[r][:, k : k + 1].to_broadcast([P, P]),
+                        rhs=identb[:],
+                        start=(r == 0),
+                        stop=(r == 1),
+                    )
             spss[i] = sps
 
         def g_op(i, grp):
@@ -416,12 +423,12 @@ def tile_hydraattention_pb_l_kernel(tc, x, mask, W_q, b_q, kv_know, kv_mask, W_o
             if half == 0:
                 y_t = sb.tile([P, 2 * KPASS], F32, tag="y", bufs=Y_BUFS, name="y")
                 ys[0] = y_t
-            nc.vector.tensor_tensor(
-                out=ys[0][:, half * KPASS : (half + 1) * KPASS],
-                in0=y_ps[:],
-                in1=bob[:, n * KPASS : (n + 1) * KPASS],
-                op=ALU.add,
-            )
+            y_half = ys[0][:, half * KPASS : (half + 1) * KPASS]
+            if n in Y_SG:
+                nc.scalar.copy(out=y_half, in_=y_ps[:])
+                nc.gpsimd.tensor_tensor(out=y_half, in0=y_half, in1=bob[:, n * KPASS : (n + 1) * KPASS], op=ALU.add)
+            else:
+                nc.vector.tensor_tensor(out=y_half, in0=y_ps[:], in1=bob[:, n * KPASS : (n + 1) * KPASS], op=ALU.add)
             if half == 1:
                 nc.sync.dma_start(out=out[b, row0 : row0 + P, (n - 1) * KPASS : (n + 1) * KPASS], in_=ys[0][:])
 
@@ -454,6 +461,8 @@ def tile_hydraattention_pb_l_kernel(tc, x, mask, W_q, b_q, kv_know, kv_mask, W_o
                 spread(steps, j, PACK)
                 if j == 1 and gt is not None:
                     g_q(gt[0], gt[1])
+            if n == 2:
+                nc.sync.dma_start(out=bob[:], in_=b_out.partition_broadcast(P))
             if n % NPASS == 1 and n // NPASS + 1 < NBLK and n > 1:
                 w_bcast(n // NPASS + 1)
             if n % NPASS == 0 and NPASS <= n <= NA:

@@ -19,40 +19,25 @@ PACK = 4
 KPASS = P * PACK
 NPASS = C // KPASS
 T = 512
+SUB = T // P
 NBLK = IMAGES * PIX // T
 BLK_PER_IMG = PIX // T
 NCT = C // P
+NSTEP = NBLK * NPASS
+
 FLOPS = 2 * 2 * IMAGES * PIX * C * C
 
-ACC_G = tuple(range(16))
-LAG = 1
 DELAY = 10
+W_OUT_CHUNKS = (1, 1, 2, 2, 2, 2, 3, 3)
+
 RAW_BUFS = 4
 IL_BUFS = 4
 U_BUFS = 3
 SQ_BUFS = 3
 QU_BUFS = 6
 Y_BUFS = 3
-S1_BUFS = 3
-S2_BUFS = 3
-QLAG = 1
-Y_SG = ()
-NMAJOR = False
-U_HEAD = ""
-ACC_HEAD = ""
-HEAD_PLAN = {
-    -1: "xvxvxvxvqsqvqsqvqsqvqsqv",
-    0: "xvqsqvqsqvxv",
-    1: "qsqvqsqvxv",
-    2: "osxv",
-    3: "osxv",
-    4: "ososxv",
-    5: "ososxv",
-    6: "ososxv",
-    7: "ososxv",
-    8: "osososxv",
-    9: "osososxv",
-}
+S1_BANKS = 3
+S2_BANKS = 3
 
 
 def tile_hydraattention_pb_l_kernel(tc, x, mask, W_q, b_q, kv_know, kv_mask, W_out, b_out, out):
@@ -66,117 +51,127 @@ def tile_hydraattention_pb_l_kernel(tc, x, mask, W_q, b_q, kv_know, kv_mask, W_o
         ps = ctx.enter_context(tc.psum_pool(name="ps", bufs=1))
         ctx.enter_context(tc.manual_schedule())
 
-        wqc = sb.tile([P, NPASS, C], U32, name="wqc", align_bytes=64)
-        wqs = sb.tile([P, C], U8, name="wqs", align_bytes=64)
-        woc = sb.tile([P, NPASS, C], U32, name="woc", align_bytes=64)
-        wos = sb.tile([P, C], U8, name="wos", align_bytes=64)
+        wq_codes = sb.tile([P, NPASS, C], U32, name="wqc", align_bytes=64)
+        wq_scales = sb.tile([P, C], U8, name="wqs", align_bytes=64)
+        wo_codes = sb.tile([P, NPASS, C], U32, name="woc", align_bytes=64)
+        wo_scales = sb.tile([P, C], U8, name="wos", align_bytes=64)
 
-        jobs = []
-        cnt = {"load": 0, "il": 0, "q": 0}
+        chunks = []
+        done = {"load": 0, "copy": 0, "quant": 0}
+        last_chunk = {}
         raws = {}
-        ils = {}
-        xcs = {}
-        xss = {}
+        interleaved = {}
+        x_codes = {}
+        x_scales = {}
 
-        def x_dst(i, g):
-            def dst():
-                if i not in xcs:
+        def x_target(i, g):
+            def target():
+                if i not in x_codes:
                     xc_t = sb.tile([P, NPASS, T], U32, tag="xc", bufs=2, align_bytes=64, name="xc")
                     xs_t = sb.tile([P, T], U8, tag="xs", bufs=2, align_bytes=64, name="xs")
-                    xcs[i] = xc_t
-                    xss[i] = xs_t
-                return xcs[i][:, g, :], xss[i][4 * g : P, :]
+                    x_codes[i] = xc_t
+                    x_scales[i] = xs_t
+                return x_codes[i][:, g, :], x_scales[i][4 * g : P, :]
 
-            return dst
+            return target
 
-        def w_dst(codes, planes, g, c0):
-            def dst():
-                return codes[:, g, c0 : c0 + KPASS], planes[4 * g : P, c0 : c0 + KPASS]
+        def w_target(codes, scales, g, c0):
+            def target():
+                return codes[:, g, c0 : c0 + KPASS], scales[4 * g : P, c0 : c0 + KPASS]
 
-            return dst
+            return target
 
-        def load_more():
-            while cnt["load"] < len(jobs) and cnt["load"] < cnt["il"] + RAW_BUFS:
-                n = cnt["load"]
+        def load_ahead():
+            while done["load"] < len(chunks) and done["load"] < done["copy"] + RAW_BUFS:
+                n = done["load"]
                 raw = sb.tile([P, PACK, KPASS], BF16, tag="raw", bufs=RAW_BUFS, name="raw")
-                nc.sync.dma_start(out=raw[:], in_=jobs[n][0].rearrange("(p j) w -> p j w", j=PACK))
+                nc.sync.dma_start(out=raw[:], in_=chunks[n][0].rearrange("(p j) w -> p j w", j=PACK))
                 raws[n] = raw
-                cnt["load"] = n + 1
+                done["load"] = n + 1
 
-        def il_next():
-            n = cnt["il"]
+        def copy_next():
+            n = done["copy"]
             raw = raws.pop(n)
             il = sb.tile([P, PACK * KPASS], BF16, tag="il", bufs=IL_BUFS, align_bytes=64, name="il")
-            if jobs[n][1]:
-                dst = il[:].rearrange("p (t m j) -> p t m j", t=PACK, j=PACK)
-                src = raw[:].rearrange("p j (m t) -> p t m j", t=PACK)
+            if chunks[n][1]:
+                dst = il[:].rearrange("p (t m j) -> p m j t", t=PACK, j=PACK)
+                src = raw[:].rearrange("p j (m t) -> p m j t", t=PACK)
             else:
-                dst = il[:].rearrange("p (w j) -> p w j", j=PACK)
-                src = raw[:].rearrange("p j w -> p w j")
-            if jobs[n][2] == "v":
+                dst = il[:].rearrange("p (c i j) -> p c j i", i=PACK, j=PACK)
+                src = raw[:].rearrange("p j (c i) -> p c j i", i=PACK)
+            if chunks[n][2] == "vector":
                 nc.vector.tensor_copy(out=dst, in_=src)
-            elif jobs[n][2] == "g":
-                nc.gpsimd.tensor_scalar(out=dst, in0=src, scalar1=1.0, scalar2=0.0, op0=ALU.mult, op1=ALU.add)
             else:
                 nc.scalar.copy(out=dst, in_=src)
-            ils[n] = il
-            cnt["il"] = n + 1
-            load_more()
+            interleaved[n] = il
+            done["copy"] = n + 1
+            load_ahead()
 
-        def q_next():
-            n = cnt["q"]
-            il = ils.pop(n)
-            codes, plane = jobs[n][3]()
-            nc.vector.quantize_mx(out=codes.bitcast(FP8X4), scales=plane, in_=il[:])
-            cnt["q"] = n + 1
+        def quantise_next():
+            n = done["quant"]
+            il = interleaved.pop(n)
+            codes, scales = chunks[n][3]()
+            nc.vector.quantize_mx(out=codes.bitcast(FP8X4), scales=scales, in_=il[:])
+            done["quant"] = n + 1
 
         def need(key):
-            while cnt["q"] <= last_job[key]:
-                if cnt["il"] <= cnt["q"]:
-                    il_next()
-                q_next()
+            while done["quant"] <= last_chunk[key]:
+                if done["copy"] <= done["quant"]:
+                    copy_next()
+                quantise_next()
 
-        def il_step():
-            il_next()
-            while cnt["q"] < cnt["il"] - QLAG:
-                q_next()
+        def chunk_step():
+            copy_next()
+            while done["quant"] < done["copy"] - 1:
+                quantise_next()
 
-        NA = NBLK * NPASS
-        head_plan = HEAD_PLAN
         x_list = [(i, g) for i in range(NBLK) for g in range(NPASS)]
-        q_list = [(grp, g) for grp in range(NPASS) for g in range(NPASS)]
-        o_list = [(n, g) for n in range(NPASS) for g in range(NPASS)]
-        last_job = {}
+        wq_list = [(grp, g) for grp in range(NPASS) for g in range(NPASS)]
+        wo_list = [(n, g) for n in range(NPASS) for g in range(NPASS)]
 
-        def add_job(kind, eng):
-            if kind == "x":
-                i, g = x_list.pop(0)
-                b = i // BLK_PER_IMG
-                t0 = (i % BLK_PER_IMG) * T
-                jobs.append((xv[b, g * KPASS : (g + 1) * KPASS, t0 : t0 + T], False, eng, x_dst(i, g)))
-                last_job[("x", i)] = len(jobs) - 1
-            elif kind == "q":
-                grp, g = q_list.pop(0)
-                src = W_q[g * KPASS : (g + 1) * KPASS, grp * KPASS : (grp + 1) * KPASS]
-                jobs.append((src, True, eng, w_dst(wqc, wqs, g, grp * KPASS)))
-                last_job[("q", grp)] = len(jobs) - 1
-            else:
-                n, g = o_list.pop(0)
-                src = W_out[g * KPASS : (g + 1) * KPASS, n * KPASS : (n + 1) * KPASS]
-                jobs.append((src, False, eng, w_dst(woc, wos, g, n * KPASS)))
-                last_job[("o", n)] = len(jobs) - 1
+        def add_x(engine):
+            i, g = x_list.pop(0)
+            b = i // BLK_PER_IMG
+            t0 = (i % BLK_PER_IMG) * T
+            chunks.append((xv[b, g * KPASS : (g + 1) * KPASS, t0 : t0 + T], False, engine, x_target(i, g)))
+            last_chunk[("x", i)] = len(chunks) - 1
 
-        n_prep = {}
-        for n in range(-1, NA):
-            if n in head_plan:
-                for r in range(len(head_plan[n]) // 2):
-                    add_job(head_plan[n][2 * r], head_plan[n][2 * r + 1])
-                n_prep[n] = len(head_plan[n]) // 2
+        def add_wq():
+            grp, g = wq_list.pop(0)
+            rows = W_q[g * KPASS : (g + 1) * KPASS, grp * KPASS : (grp + 1) * KPASS]
+            engine = "scalar" if g % 2 == 0 else "vector"
+            chunks.append((rows, True, engine, w_target(wq_codes, wq_scales, g, grp * KPASS)))
+            last_chunk[("wq", grp)] = len(chunks) - 1
+
+        def add_wo():
+            n, g = wo_list.pop(0)
+            rows = W_out[g * KPASS : (g + 1) * KPASS, n * KPASS : (n + 1) * KPASS]
+            chunks.append((rows, False, "scalar", w_target(wo_codes, wo_scales, g, n * KPASS)))
+            last_chunk[("wo", n)] = len(chunks) - 1
+
+        chunks_of_step = {}
+        for n in range(-1, NSTEP):
+            first = len(chunks)
+            if n == -1:
+                for r in range(NPASS):
+                    add_x("vector")
+                for r in range(2 * NPASS):
+                    add_wq()
+            elif n < DELAY:
+                if n == 0:
+                    add_x("vector")
+                if n < 2:
+                    for r in range(NPASS):
+                        add_wq()
+                else:
+                    for r in range(W_OUT_CHUNKS[n - 2]):
+                        add_wo()
+                add_x("vector")
             elif x_list:
-                add_job("x", "s")
-                n_prep[n] = 1
+                add_x("scalar")
+            chunks_of_step[n] = len(chunks) - first
 
-        load_more()
+        load_ahead()
 
         mrow = sb.tile([P, P], BF16, name="mrow")
         nc.vector.memset(mrow[:], 0.0)
@@ -187,7 +182,7 @@ def tile_hydraattention_pb_l_kernel(tc, x, mask, W_q, b_q, kv_know, kv_mask, W_o
         nc.scalar.dma_start(out=kk_r[:], in_=kv_know.rearrange("b o (g p j) -> p (b o g) j", p=P, j=PACK))
         km_r = sb.tile([P, IMAGES * NPASS, PACK], BF16, name="km_r")
         nc.scalar.dma_start(out=km_r[:], in_=kv_mask.rearrange("b o (g p j) -> p (b o g) j", p=P, j=PACK))
-        bob = sb.tile([P, C], BF16, name="bob")
+        b_out_all = sb.tile([P, C], BF16, name="bob")
 
         warm = sb.tile([P, 1], F32, name="warm")
         nc.vector.memset(warm[:], 1.0)
@@ -196,12 +191,12 @@ def tile_hydraattention_pb_l_kernel(tc, x, mask, W_q, b_q, kv_know, kv_mask, W_o
 
         ones2 = sb.tile([P, 2], F32, name="ones2")
         nc.vector.memset(ones2[:], 1.0)
-        identb = sb.tile([P, P], BF16, name="identb")
-        make_identity(nc, identb[:])
-        identf = sb.tile([P, P], F32, name="identf")
-        make_identity(nc, identf[:])
+        ident_bf = sb.tile([P, P], BF16, name="identb")
+        make_identity(nc, ident_bf[:])
+        ident_f32 = sb.tile([P, P], F32, name="identf")
+        make_identity(nc, ident_f32[:])
 
-        def const_math():
+        def constants():
             bq = sb.tile([P, NCT], F32, name="bq")
             nc.vector.tensor_copy(out=bq[:], in_=bq_r[:].rearrange("p g j -> p (g j)"))
             kvk = sb.tile([P, IMAGES * NCT], F32, name="kvk")
@@ -229,257 +224,206 @@ def tile_hydraattention_pb_l_kernel(tc, x, mask, W_q, b_q, kv_know, kv_mask, W_o
             nc.vector.reciprocal(out=rsig[:], in_=sig_r[:])
             w_r = sb.tile([P, P], F32, name="w_r")
             nc.vector.tensor_tensor(out=w_r[:], in0=cb[:], in1=rsig[:], op=ALU.mult)
-            nchunk = IMAGES * PIX // P
-            nc.sync.dma_start(out=park.rearrange("r (c p) -> (r c) p", p=P), in_=w_r[0:nchunk, :])
+            nrows = IMAGES * PIX // P
+            nc.sync.dma_start(out=park.rearrange("r (c p) -> (r c) p", p=P), in_=w_r[0:nrows, :])
             s_ps = ps.tile([P, P], F32, tag="misc", bufs=1, name="s_ps")
-            nc.tensor.transpose(out=s_ps[:], in_=sig_r[:], identity=identf[:])
-            sig = sb.tile([P, nchunk], F32, name="sig")
-            nc.vector.tensor_copy(out=sig[:], in_=s_ps[:, 0:nchunk])
-            return bq, kvk, dk, sig
+            nc.tensor.transpose(out=s_ps[:], in_=sig_r[:], identity=ident_f32[:])
+            sigma = sb.tile([P, nrows], F32, name="sig")
+            nc.vector.tensor_copy(out=sigma[:], in_=s_ps[:, 0:nrows])
+            return bq, kvk, dk, sigma
 
-        wbs = {}
-        us = {}
-        qus = {}
-        accs = {}
-        npss = {}
-        scs = {}
-        spss = {}
-        gis = {}
-        gcs = {}
-        gss = {}
-        ys = {}
+        w_all = {}
+        u_tiles = {}
+        qu_tiles = {}
+        sums = {}
+        norms = {}
+        s_parts = {}
+        s_all = {}
+        g_tiles = {}
+        g_codes = {}
+        g_scales = {}
+        y_tiles = {}
 
-        def w_bcast(i):
+        def load_w(i):
             wb = sb.tile([P, T], F32, tag="wb", bufs=2, name="wb")
             per_row = C // T
             src = park[i // per_row, (i % per_row) * T : (i % per_row + 1) * T]
             nc.sync.dma_start(out=wb[:], in_=src.partition_broadcast(P))
-            wbs[i] = wb
+            w_all[i] = wb
 
-        def u_tile(n):
-            if n in us or n >= NBLK * NCT:
+        def make_u(n):
+            if n in u_tiles or n >= NBLK * NCT:
                 return
             i = n // NCT
             col = (i // BLK_PER_IMG) * NCT + n % NCT
             u = sb.tile([P, T], F32, tag="u", bufs=U_BUFS, name="u")
-            ue = U_HEAD[n // PACK] if n // PACK < len(U_HEAD) else "s"
-            if ue == "g":
-                nc.gpsimd.tensor_scalar(
-                    out=u[:],
-                    in0=wbs[i][:],
-                    scalar1=dk[:, col : col + 1],
-                    scalar2=kvk[:, col : col + 1],
-                    op0=ALU.mult,
-                    op1=ALU.add,
-                )
-            elif ue == "v":
-                nc.vector.tensor_scalar(
-                    out=u[:],
-                    in0=wbs[i][:],
-                    scalar1=dk[:, col : col + 1],
-                    scalar2=kvk[:, col : col + 1],
-                    op0=ALU.mult,
-                    op1=ALU.add,
-                )
-            else:
-                nc.scalar.activation(
-                    out=u[:], in_=wbs[i][:], func=ACT.Identity, bias=kvk[:, col : col + 1], scale=dk[:, col : col + 1]
-                )
-            us[n] = u
+            nc.scalar.activation(
+                out=u[:], in_=w_all[i][:], func=ACT.Identity, bias=kvk[:, col : col + 1], scale=dk[:, col : col + 1]
+            )
+            u_tiles[n] = u
 
-        def a_tile(i, ct):
+        def stage1_tile(i, ct):
             n = i * NCT + ct
             grp = ct // PACK
             j = ct % PACK
             need(("x", i))
-            need(("q", grp))
-            u_tile(n)
-            acc_ps = ps.tile([P, T], F32, tag="s1", bufs=S1_BUFS, name="s1")
+            need(("wq", grp))
+            make_u(n)
+            q_ps = ps.tile([P, T], F32, tag="s1", bufs=S1_BANKS, name="s1")
             for g in range(NPASS):
                 nc.tensor.matmul_mx(
-                    out=acc_ps[:],
-                    lhsT=wqc[:, g, ct * P : (ct + 1) * P].bitcast(FP8X4),
-                    lhsT_scale=wqs[4 * g : P, ct * P : (ct + 1) * P],
-                    rhs=xcs[i][:, g, :].bitcast(FP8X4),
-                    rhs_scale=xss[i][4 * g : P, :],
+                    out=q_ps[:],
+                    lhsT=wq_codes[:, g, ct * P : (ct + 1) * P].bitcast(FP8X4),
+                    lhsT_scale=wq_scales[4 * g : P, ct * P : (ct + 1) * P],
+                    rhs=x_codes[i][:, g, :].bitcast(FP8X4),
+                    rhs_scale=x_scales[i][4 * g : P, :],
                     start=(g == 0),
                     stop=(g == NPASS - 1),
                 )
-            u_tile(n + 1)
-            eng = "g" if ct in ACC_G else "v"
-            if n // PACK < len(ACC_HEAD):
-                eng = ACC_HEAD[n // PACK]
-            first = (i, eng) not in accs
+            make_u(n + 1)
+            first = i not in sums
             if first:
-                sq = sb.tile([P, T], F32, tag="acc%s" % eng, bufs=2, name="acc%s" % eng)
-                accs[(i, eng)] = sq
+                sq = sb.tile([P, T], F32, tag="accg", bufs=2, name="accg")
+                sums[i] = sq
             else:
                 sq = sb.tile([P, T], F32, tag="sq", bufs=SQ_BUFS, name="sq")
-            nc.scalar.activation(out=sq[:], in_=acc_ps[:], func=ACT.Square, bias=bq[:, ct : ct + 1], scale=1.0)
+            nc.scalar.activation(out=sq[:], in_=q_ps[:], func=ACT.Square, bias=bq[:, ct : ct + 1], scale=1.0)
             if j == 0:
                 qu_t = sb.tile([P, PACK, T], F32, tag="qu", bufs=QU_BUFS, name="qu")
-                qus[(i, grp)] = qu_t
+                qu_tiles[(i, grp)] = qu_t
             nc.vector.scalar_tensor_tensor(
-                out=qus[(i, grp)][:, j, :],
-                in0=acc_ps[:],
+                out=qu_tiles[(i, grp)][:, j, :],
+                in0=q_ps[:],
                 scalar=bq[:, ct : ct + 1],
-                in1=us.pop(n)[:],
+                in1=u_tiles.pop(n)[:],
                 op0=ALU.add,
                 op1=ALU.mult,
             )
             if not first:
-                a = accs[(i, eng)]
-                if eng == "g":
-                    nc.gpsimd.tensor_tensor(out=a[:], in0=a[:], in1=sq[:], op=ALU.add)
-                else:
-                    nc.vector.tensor_tensor(out=a[:], in0=a[:], in1=sq[:], op=ALU.add)
+                nc.gpsimd.tensor_tensor(out=sums[i][:], in0=sums[i][:], in1=sq[:], op=ALU.add)
 
-        def norm_pe(i):
-            nps = ps.tile([P, 2 * (T // P)], F32, tag="misc", bufs=1, name="nps")
-            parts = [accs.pop((i, e)) for e in ("v", "g") if (i, e) in accs]
-            for k in range(T // P):
-                for r in range(len(parts)):
-                    nc.tensor.matmul(
-                        out=nps[:, 2 * k : 2 * k + 2],
-                        lhsT=parts[r][:, k * P : (k + 1) * P],
-                        rhs=ones2[:],
-                        start=(r == 0),
-                        stop=(r == len(parts) - 1),
-                    )
-            nrm = sb.tile([P, T // P], F32, tag="nrm", bufs=2, name="nrm")
-            nc.scalar.activation(out=nrm[:], in_=nps[:].rearrange("p (k two) -> p k two", two=2)[:, :, 0], func=ACT.Sqrt)
-            npss[i] = nrm
-
-        def norm_small(i):
-            nrm = npss.pop(i)
-            rn = sb.tile([P, T // P], F32, tag="rn", bufs=2, name="rn")
+        def norm(i):
+            n_ps = ps.tile([P, 2 * SUB], F32, tag="misc", bufs=1, name="nps")
+            total = sums.pop(i)
+            for k in range(SUB):
+                nc.tensor.matmul(
+                    out=n_ps[:, 2 * k : 2 * k + 2], lhsT=total[:, k * P : (k + 1) * P], rhs=ones2[:], start=True, stop=True
+                )
+            nrm = sb.tile([P, SUB], F32, tag="nrm", bufs=2, name="nrm")
+            nc.scalar.activation(out=nrm[:], in_=n_ps[:].rearrange("p (k two) -> p k two", two=2)[:, :, 0], func=ACT.Sqrt)
+            rn = sb.tile([P, SUB], F32, tag="rn", bufs=2, name="rn")
             nc.vector.reciprocal(out=rn[:], in_=nrm[:])
-            sc = sb.tile([P, T // P], F32, tag="sc", bufs=2, name="sc")
-            c0 = i * (T // P)
-            nc.vector.tensor_tensor(out=sc[:], in0=rn[:], in1=sig[:, c0 : c0 + T // P], op=ALU.mult)
-            s_hi = sb.tile([P, T // P], BF16, tag="s_hi", bufs=2, name="s_hi")
+            sc = sb.tile([P, SUB], F32, tag="sc", bufs=2, name="sc")
+            nc.vector.tensor_tensor(out=sc[:], in0=rn[:], in1=sigma[:, i * SUB : (i + 1) * SUB], op=ALU.mult)
+            s_hi = sb.tile([P, SUB], BF16, tag="s_hi", bufs=2, name="s_hi")
             nc.vector.tensor_copy(out=s_hi[:], in_=sc[:])
-            s_lo = sb.tile([P, T // P], BF16, tag="s_lo", bufs=2, name="s_lo")
+            s_lo = sb.tile([P, SUB], BF16, tag="s_lo", bufs=2, name="s_lo")
             nc.vector.tensor_tensor(out=s_lo[:], in0=sc[:], in1=s_hi[:], op=ALU.subtract)
-            scs[i] = (s_hi, s_lo)
+            s_parts[i] = (s_hi, s_lo)
 
-        def s_bcast(i):
-            sc = scs.pop(i)
-            sps = ps.tile([P, T], F32, tag="sps", bufs=1, name="sps")
-            for k in range(T // P):
+        def spread_s(i):
+            parts = s_parts.pop(i)
+            s_ps = ps.tile([P, T], F32, tag="sps", bufs=1, name="sps")
+            for k in range(SUB):
                 for r in range(2):
                     nc.tensor.matmul(
-                        out=sps[:, k * P : (k + 1) * P],
-                        lhsT=sc[r][:, k : k + 1].to_broadcast([P, P]),
-                        rhs=identb[:],
+                        out=s_ps[:, k * P : (k + 1) * P],
+                        lhsT=parts[r][:, k : k + 1].to_broadcast([P, P]),
+                        rhs=ident_bf[:],
                         start=(r == 0),
                         stop=(r == 1),
                     )
-            spss[i] = sps
+            s_all[i] = s_ps
 
-        def g_op(i, grp):
+        def make_g(i, grp):
             gi = sb.tile([P, T, PACK], BF16, tag="gi", bufs=2, align_bytes=64, name="gi")
             nc.vector.tensor_tensor(
                 out=gi[:],
-                in0=qus.pop((i, grp))[:].rearrange("p j t -> p t j"),
-                in1=spss[i][:].unsqueeze(2).to_broadcast([P, T, PACK]),
+                in0=qu_tiles.pop((i, grp))[:].rearrange("p j t -> p t j"),
+                in1=s_all[i][:].unsqueeze(2).to_broadcast([P, T, PACK]),
                 op=ALU.mult,
             )
-            gis[(i, grp)] = gi
+            g_tiles[(i, grp)] = gi
 
-        def g_q(i, grp):
-            if i not in gcs:
-                gc_t = sb.tile([P, NPASS, T], U32, tag="gc", bufs=LAG + 1, align_bytes=64, name="gc")
-                gs_t = sb.tile([P, T], U8, tag="gs", bufs=LAG + 1, align_bytes=64, name="gs")
-                gcs[i] = gc_t
-                gss[i] = gs_t
+        def quantise_g(i, grp):
+            if i not in g_codes:
+                gc_t = sb.tile([P, NPASS, T], U32, tag="gc", bufs=2, align_bytes=64, name="gc")
+                gs_t = sb.tile([P, T], U8, tag="gs", bufs=2, align_bytes=64, name="gs")
+                g_codes[i] = gc_t
+                g_scales[i] = gs_t
             nc.vector.quantize_mx(
-                out=gcs[i][:, grp, :].bitcast(FP8X4),
-                scales=gss[i][4 * grp : P, :],
-                in_=gis.pop((i, grp))[:].rearrange("p t j -> p (t j)"),
+                out=g_codes[i][:, grp, :].bitcast(FP8X4),
+                scales=g_scales[i][4 * grp : P, :],
+                in_=g_tiles.pop((i, grp))[:].rearrange("p t j -> p (t j)"),
             )
 
-        def b_bank(k, tt, n):
-            b = k // BLK_PER_IMG
-            row0 = (k % BLK_PER_IMG) * T + tt * P
-            need(("o", n))
-            y_ps = ps.tile([P, KPASS], F32, tag="s2", bufs=S2_BUFS, name="s2")
+        def stage2_bank(i, tt, n):
+            b = i // BLK_PER_IMG
+            row0 = (i % BLK_PER_IMG) * T + tt * P
+            need(("wo", n))
+            y_ps = ps.tile([P, KPASS], F32, tag="s2", bufs=S2_BANKS, name="s2")
             for g in range(NPASS):
                 nc.tensor.matmul_mx(
                     out=y_ps[:],
-                    lhsT=gcs[k][:, g, tt * P : (tt + 1) * P].bitcast(FP8X4),
-                    lhsT_scale=gss[k][4 * g : P, tt * P : (tt + 1) * P],
-                    rhs=woc[:, g, n * KPASS : (n + 1) * KPASS].bitcast(FP8X4),
-                    rhs_scale=wos[4 * g : P, n * KPASS : (n + 1) * KPASS],
+                    lhsT=g_codes[i][:, g, tt * P : (tt + 1) * P].bitcast(FP8X4),
+                    lhsT_scale=g_scales[i][4 * g : P, tt * P : (tt + 1) * P],
+                    rhs=wo_codes[:, g, n * KPASS : (n + 1) * KPASS].bitcast(FP8X4),
+                    rhs_scale=wo_scales[4 * g : P, n * KPASS : (n + 1) * KPASS],
                     start=(g == 0),
                     stop=(g == NPASS - 1),
                 )
-            if NMAJOR:
-                y_t = sb.tile([P, KPASS], F32, tag="y", bufs=Y_BUFS, name="y")
-                nc.vector.tensor_tensor(out=y_t[:], in0=y_ps[:], in1=bob[:, n * KPASS : (n + 1) * KPASS], op=ALU.add)
-                nc.sync.dma_start(out=out[b, row0 : row0 + P, n * KPASS : (n + 1) * KPASS], in_=y_t[:])
-                return
             half = n % 2
             if half == 0:
                 y_t = sb.tile([P, 2 * KPASS], F32, tag="y", bufs=Y_BUFS, name="y")
-                ys[0] = y_t
-            y_half = ys[0][:, half * KPASS : (half + 1) * KPASS]
-            if n in Y_SG:
-                nc.scalar.copy(out=y_half, in_=y_ps[:])
-                nc.gpsimd.tensor_tensor(out=y_half, in0=y_half, in1=bob[:, n * KPASS : (n + 1) * KPASS], op=ALU.add)
-            else:
-                nc.vector.tensor_tensor(out=y_half, in0=y_ps[:], in1=bob[:, n * KPASS : (n + 1) * KPASS], op=ALU.add)
+                y_tiles[0] = y_t
+            nc.vector.tensor_tensor(
+                out=y_tiles[0][:, half * KPASS : (half + 1) * KPASS],
+                in0=y_ps[:],
+                in1=b_out_all[:, n * KPASS : (n + 1) * KPASS],
+                op=ALU.add,
+            )
             if half == 1:
-                nc.sync.dma_start(out=out[b, row0 : row0 + P, (n - 1) * KPASS : (n + 1) * KPASS], in_=ys[0][:])
+                nc.sync.dma_start(out=out[b, row0 : row0 + P, (n - 1) * KPASS : (n + 1) * KPASS], in_=y_tiles[0][:])
 
         g_ready = []
 
-        def prep_steps(k):
-            return [il_step for r in range(k)]
+        def share(steps, pos, npos):
+            for r in range(steps * pos // npos, steps * (pos + 1) // npos):
+                chunk_step()
 
-        def spread(steps, pos, npos):
-            lo = len(steps) * pos // npos
-            hi = len(steps) * (pos + 1) // npos
-            for f in steps[lo:hi]:
-                f()
-
-        def pair(n):
-            steps = prep_steps(n_prep.get(n, 0))
-            gt = g_ready.pop(0) if g_ready else None
-            if steps:
-                steps.pop(0)()
-            if gt is not None:
-                g_op(gt[0], gt[1])
+        def step(n):
+            steps = chunks_of_step.get(n, 0)
+            todo = g_ready.pop(0) if g_ready else None
+            if steps > 0:
+                chunk_step()
+                steps = steps - 1
+            if todo is not None:
+                make_g(todo[0], todo[1])
             for j in range(PACK):
-                if n < NA:
-                    a_tile(n // NPASS, (n % NPASS) * PACK + j)
+                if n < NSTEP:
+                    stage1_tile(n // NPASS, (n % NPASS) * PACK + j)
                 if n >= DELAY:
-                    if NMAJOR:
-                        b_bank((n - DELAY) // 4, j, (n - DELAY) % 4)
-                    else:
-                        b_bank((n - DELAY) // 4, (n - DELAY) % 4, j)
-                spread(steps, j, PACK)
-                if j == 1 and gt is not None:
-                    g_q(gt[0], gt[1])
+                    stage2_bank((n - DELAY) // SUB, (n - DELAY) % SUB, j)
+                share(steps, j, PACK)
+                if j == 1 and todo is not None:
+                    quantise_g(todo[0], todo[1])
             if n == 2:
-                nc.sync.dma_start(out=bob[:], in_=b_out.partition_broadcast(P))
+                nc.sync.dma_start(out=b_out_all[:], in_=b_out.partition_broadcast(P))
             if n % NPASS == 1 and n // NPASS + 1 < NBLK and n > 1:
-                w_bcast(n // NPASS + 1)
-            if n % NPASS == 0 and NPASS <= n <= NA:
-                norm_pe(n // NPASS - 1)
-                norm_small(n // NPASS - 1)
-            if n % NPASS == 1 and NPASS <= n <= NA + 1:
+                load_w(n // NPASS + 1)
+            if n % NPASS == 0 and NPASS <= n <= NSTEP:
+                norm(n // NPASS - 1)
+            if n % NPASS == 1 and NPASS <= n <= NSTEP + 1:
                 i = n // NPASS - 1
-                s_bcast(i)
+                spread_s(i)
                 for grp in range(NPASS):
                     g_ready.append((i, grp))
 
-        steps = prep_steps(n_prep[-1])
-        spread(steps, 0, 3)
-        bq, kvk, dk, sig = const_math()
-        spread(steps, 1, 3)
-        w_bcast(0)
-        spread(steps, 2, 3)
-        w_bcast(1)
-        for n in range(NA + DELAY):
-            pair(n)
+        share(chunks_of_step[-1], 0, 3)
+        bq, kvk, dk, sigma = constants()
+        share(chunks_of_step[-1], 1, 3)
+        load_w(0)
+        share(chunks_of_step[-1], 2, 3)
+        load_w(1)
+        for n in range(NSTEP + DELAY):
+            step(n)

@@ -44,7 +44,7 @@ def tile_hydraattention_pb_l_kernel(tc, x, mask, W_q, b_q, kv_know, kv_mask, W_o
     nc = tc.nc
     xv = x.rearrange("b c h w -> b c (h w)")
     park = out[IMAGES - 1, PIX - IMAGES * PIX // C : PIX, :]
-    mrows = mask.rearrange("b o h w -> (b o h w)").rearrange("(c p) -> c p", p=P)
+    mask_rows = mask.rearrange("b o h w -> (b o h w)").rearrange("(c p) -> c p", p=P)
 
     with ExitStack() as ctx:
         sb = ctx.enter_context(tc.tile_pool(name="sb", bufs=1))
@@ -83,36 +83,36 @@ def tile_hydraattention_pb_l_kernel(tc, x, mask, W_q, b_q, kv_know, kv_mask, W_o
 
         def load_ahead():
             while done["load"] < len(chunks) and done["load"] < done["copy"] + RAW_BUFS:
-                n = done["load"]
+                ci = done["load"]
                 raw = sb.tile([P, PACK, KPASS], BF16, tag="raw", bufs=RAW_BUFS, name="raw")
-                nc.sync.dma_start(out=raw[:], in_=chunks[n][0].rearrange("(p j) w -> p j w", j=PACK))
-                raws[n] = raw
-                done["load"] = n + 1
+                nc.sync.dma_start(out=raw[:], in_=chunks[ci][0].rearrange("(p j) w -> p j w", j=PACK))
+                raws[ci] = raw
+                done["load"] = ci + 1
 
         def copy_next():
-            n = done["copy"]
-            raw = raws.pop(n)
+            ci = done["copy"]
+            raw = raws.pop(ci)
             il = sb.tile([P, PACK * KPASS], BF16, tag="il", bufs=IL_BUFS, align_bytes=64, name="il")
-            if chunks[n][1]:
+            if chunks[ci][1]:
                 dst = il[:].rearrange("p (t m j) -> p m j t", t=PACK, j=PACK)
                 src = raw[:].rearrange("p j (m t) -> p m j t", t=PACK)
             else:
                 dst = il[:].rearrange("p (c i j) -> p c j i", i=PACK, j=PACK)
                 src = raw[:].rearrange("p j (c i) -> p c j i", i=PACK)
-            if chunks[n][2] == "vector":
+            if chunks[ci][2] == "vector":
                 nc.vector.tensor_copy(out=dst, in_=src)
             else:
                 nc.scalar.copy(out=dst, in_=src)
-            interleaved[n] = il
-            done["copy"] = n + 1
+            interleaved[ci] = il
+            done["copy"] = ci + 1
             load_ahead()
 
         def quantise_next():
-            n = done["quant"]
-            il = interleaved.pop(n)
-            codes, scales = chunks[n][3]()
+            ci = done["quant"]
+            il = interleaved.pop(ci)
+            codes, scales = chunks[ci][3]()
             nc.vector.quantize_mx(out=codes.bitcast(FP8X4), scales=scales, in_=il[:])
-            done["quant"] = n + 1
+            done["quant"] = ci + 1
 
         def need(key):
             while done["quant"] <= last_chunk[key]:
@@ -127,7 +127,7 @@ def tile_hydraattention_pb_l_kernel(tc, x, mask, W_q, b_q, kv_know, kv_mask, W_o
 
         x_list = [(i, g) for i in range(NBLK) for g in range(NPASS)]
         wq_list = [(grp, g) for grp in range(NPASS) for g in range(NPASS)]
-        wo_list = [(n, g) for n in range(NPASS) for g in range(NPASS)]
+        wo_list = [(col, g) for col in range(NPASS) for g in range(NPASS)]
 
         def add_x(engine):
             i, g = x_list.pop(0)
@@ -144,38 +144,38 @@ def tile_hydraattention_pb_l_kernel(tc, x, mask, W_q, b_q, kv_know, kv_mask, W_o
             last_chunk[("wq", grp)] = len(chunks) - 1
 
         def add_wo():
-            n, g = wo_list.pop(0)
-            rows = W_out[g * KPASS : (g + 1) * KPASS, n * KPASS : (n + 1) * KPASS]
-            chunks.append((rows, False, "scalar", w_target(wo_codes, wo_scales, g, n * KPASS)))
-            last_chunk[("wo", n)] = len(chunks) - 1
+            col, g = wo_list.pop(0)
+            rows = W_out[g * KPASS : (g + 1) * KPASS, col * KPASS : (col + 1) * KPASS]
+            chunks.append((rows, False, "scalar", w_target(wo_codes, wo_scales, g, col * KPASS)))
+            last_chunk[("wo", col)] = len(chunks) - 1
 
         chunks_of_step = {}
-        for n in range(-1, NSTEP):
-            first = len(chunks)
-            if n == -1:
+        for st in range(-1, NSTEP):
+            before = len(chunks)
+            if st == -1:
                 for r in range(NPASS):
                     add_x("vector")
                 for r in range(2 * NPASS):
                     add_wq()
-            elif n < DELAY:
-                if n == 0:
+            elif st < DELAY:
+                if st == 0:
                     add_x("vector")
-                if n < 2:
+                if st < 2:
                     for r in range(NPASS):
                         add_wq()
                 else:
-                    for r in range(W_OUT_CHUNKS[n - 2]):
+                    for r in range(W_OUT_CHUNKS[st - 2]):
                         add_wo()
                 add_x("vector")
             elif x_list:
                 add_x("scalar")
-            chunks_of_step[n] = len(chunks) - first
+            chunks_of_step[st] = len(chunks) - before
 
         load_ahead()
 
         mrow = sb.tile([P, P], BF16, name="mrow")
         nc.vector.memset(mrow[:], 0.0)
-        nc.scalar.dma_start(out=mrow[0:64, :], in_=mrows)
+        nc.scalar.dma_start(out=mrow[0:64, :], in_=mask_rows)
         bq_r = sb.tile([P, NPASS, PACK], BF16, name="bq_r")
         nc.scalar.dma_start(out=bq_r[:], in_=b_q.rearrange("(g p j) -> p g j", p=P, j=PACK))
         kk_r = sb.tile([P, IMAGES * NPASS, PACK], BF16, name="kk_r")
@@ -226,23 +226,22 @@ def tile_hydraattention_pb_l_kernel(tc, x, mask, W_q, b_q, kv_know, kv_mask, W_o
             nc.vector.tensor_tensor(out=w_r[:], in0=cb[:], in1=rsig[:], op=ALU.mult)
             nrows = IMAGES * PIX // P
             nc.sync.dma_start(out=park.rearrange("r (c p) -> (r c) p", p=P), in_=w_r[0:nrows, :])
-            s_ps = ps.tile([P, P], F32, tag="misc", bufs=1, name="s_ps")
-            nc.tensor.transpose(out=s_ps[:], in_=sig_r[:], identity=ident_f32[:])
+            sig_ps = ps.tile([P, P], F32, tag="misc", bufs=1, name="s_ps")
+            nc.tensor.transpose(out=sig_ps[:], in_=sig_r[:], identity=ident_f32[:])
             sigma = sb.tile([P, nrows], F32, name="sig")
-            nc.vector.tensor_copy(out=sigma[:], in_=s_ps[:, 0:nrows])
+            nc.vector.tensor_copy(out=sigma[:], in_=sig_ps[:, 0:nrows])
             return bq, kvk, dk, sigma
 
         w_all = {}
         u_tiles = {}
         qu_tiles = {}
         sums = {}
-        norms = {}
         s_parts = {}
         s_all = {}
         g_tiles = {}
         g_codes = {}
         g_scales = {}
-        y_tiles = {}
+        y_open = []
 
         def load_w(i):
             wb = sb.tile([P, T], F32, tag="wb", bufs=2, name="wb")
@@ -251,24 +250,24 @@ def tile_hydraattention_pb_l_kernel(tc, x, mask, W_q, b_q, kv_know, kv_mask, W_o
             nc.sync.dma_start(out=wb[:], in_=src.partition_broadcast(P))
             w_all[i] = wb
 
-        def make_u(n):
-            if n in u_tiles or n >= NBLK * NCT:
+        def make_u(tile_no):
+            if tile_no in u_tiles or tile_no >= NBLK * NCT:
                 return
-            i = n // NCT
-            col = (i // BLK_PER_IMG) * NCT + n % NCT
+            i = tile_no // NCT
+            v = (i // BLK_PER_IMG) * NCT + tile_no % NCT
             u = sb.tile([P, T], F32, tag="u", bufs=U_BUFS, name="u")
             nc.scalar.activation(
-                out=u[:], in_=w_all[i][:], func=ACT.Identity, bias=kvk[:, col : col + 1], scale=dk[:, col : col + 1]
+                out=u[:], in_=w_all[i][:], func=ACT.Identity, bias=kvk[:, v : v + 1], scale=dk[:, v : v + 1]
             )
-            u_tiles[n] = u
+            u_tiles[tile_no] = u
 
         def stage1_tile(i, ct):
-            n = i * NCT + ct
+            tile_no = i * NCT + ct
             grp = ct // PACK
             j = ct % PACK
             need(("x", i))
             need(("wq", grp))
-            make_u(n)
+            make_u(tile_no)
             q_ps = ps.tile([P, T], F32, tag="s1", bufs=S1_BANKS, name="s1")
             for g in range(NPASS):
                 nc.tensor.matmul_mx(
@@ -280,9 +279,9 @@ def tile_hydraattention_pb_l_kernel(tc, x, mask, W_q, b_q, kv_know, kv_mask, W_o
                     start=(g == 0),
                     stop=(g == NPASS - 1),
                 )
-            make_u(n + 1)
-            first = i not in sums
-            if first:
+            make_u(tile_no + 1)
+            opens_sum = i not in sums
+            if opens_sum:
                 sq = sb.tile([P, T], F32, tag="accg", bufs=2, name="accg")
                 sums[i] = sq
             else:
@@ -295,19 +294,23 @@ def tile_hydraattention_pb_l_kernel(tc, x, mask, W_q, b_q, kv_know, kv_mask, W_o
                 out=qu_tiles[(i, grp)][:, j, :],
                 in0=q_ps[:],
                 scalar=bq[:, ct : ct + 1],
-                in1=u_tiles.pop(n)[:],
+                in1=u_tiles.pop(tile_no)[:],
                 op0=ALU.add,
                 op1=ALU.mult,
             )
-            if not first:
+            if not opens_sum:
                 nc.gpsimd.tensor_tensor(out=sums[i][:], in0=sums[i][:], in1=sq[:], op=ALU.add)
 
         def norm(i):
             n_ps = ps.tile([P, 2 * SUB], F32, tag="misc", bufs=1, name="nps")
             total = sums.pop(i)
-            for k in range(SUB):
+            for tt in range(SUB):
                 nc.tensor.matmul(
-                    out=n_ps[:, 2 * k : 2 * k + 2], lhsT=total[:, k * P : (k + 1) * P], rhs=ones2[:], start=True, stop=True
+                    out=n_ps[:, 2 * tt : 2 * tt + 2],
+                    lhsT=total[:, tt * P : (tt + 1) * P],
+                    rhs=ones2[:],
+                    start=True,
+                    stop=True,
                 )
             nrm = sb.tile([P, SUB], F32, tag="nrm", bufs=2, name="nrm")
             nc.scalar.activation(out=nrm[:], in_=n_ps[:].rearrange("p (k two) -> p k two", two=2)[:, :, 0], func=ACT.Sqrt)
@@ -324,11 +327,11 @@ def tile_hydraattention_pb_l_kernel(tc, x, mask, W_q, b_q, kv_know, kv_mask, W_o
         def spread_s(i):
             parts = s_parts.pop(i)
             s_ps = ps.tile([P, T], F32, tag="sps", bufs=1, name="sps")
-            for k in range(SUB):
+            for tt in range(SUB):
                 for r in range(2):
                     nc.tensor.matmul(
-                        out=s_ps[:, k * P : (k + 1) * P],
-                        lhsT=parts[r][:, k : k + 1].to_broadcast([P, P]),
+                        out=s_ps[:, tt * P : (tt + 1) * P],
+                        lhsT=parts[r][:, tt : tt + 1].to_broadcast([P, P]),
                         rhs=ident_bf[:],
                         start=(r == 0),
                         stop=(r == 1),
@@ -338,9 +341,9 @@ def tile_hydraattention_pb_l_kernel(tc, x, mask, W_q, b_q, kv_know, kv_mask, W_o
         def make_g(i, grp):
             gi = sb.tile([P, T, PACK], BF16, tag="gi", bufs=2, align_bytes=64, name="gi")
             nc.vector.tensor_tensor(
-                out=gi[:],
-                in0=qu_tiles.pop((i, grp))[:].rearrange("p j t -> p t j"),
-                in1=s_all[i][:].unsqueeze(2).to_broadcast([P, T, PACK]),
+                out=gi[:].rearrange("p (c i) j -> p c j i", i=PACK),
+                in0=qu_tiles.pop((i, grp))[:].rearrange("p j (c i) -> p c j i", i=PACK),
+                in1=s_all[i][:].rearrange("p (c i) -> p c i", i=PACK).unsqueeze(2).to_broadcast([P, T // PACK, PACK, PACK]),
                 op=ALU.mult,
             )
             g_tiles[(i, grp)] = gi
@@ -357,64 +360,66 @@ def tile_hydraattention_pb_l_kernel(tc, x, mask, W_q, b_q, kv_know, kv_mask, W_o
                 in_=g_tiles.pop((i, grp))[:].rearrange("p t j -> p (t j)"),
             )
 
-        def stage2_bank(i, tt, n):
+        def stage2_bank(i, tt, col):
             b = i // BLK_PER_IMG
             row0 = (i % BLK_PER_IMG) * T + tt * P
-            need(("wo", n))
+            need(("wo", col))
             y_ps = ps.tile([P, KPASS], F32, tag="s2", bufs=S2_BANKS, name="s2")
             for g in range(NPASS):
                 nc.tensor.matmul_mx(
                     out=y_ps[:],
                     lhsT=g_codes[i][:, g, tt * P : (tt + 1) * P].bitcast(FP8X4),
                     lhsT_scale=g_scales[i][4 * g : P, tt * P : (tt + 1) * P],
-                    rhs=wo_codes[:, g, n * KPASS : (n + 1) * KPASS].bitcast(FP8X4),
-                    rhs_scale=wo_scales[4 * g : P, n * KPASS : (n + 1) * KPASS],
+                    rhs=wo_codes[:, g, col * KPASS : (col + 1) * KPASS].bitcast(FP8X4),
+                    rhs_scale=wo_scales[4 * g : P, col * KPASS : (col + 1) * KPASS],
                     start=(g == 0),
                     stop=(g == NPASS - 1),
                 )
-            half = n % 2
+            half = col % 2
             if half == 0:
                 y_t = sb.tile([P, 2 * KPASS], F32, tag="y", bufs=Y_BUFS, name="y")
-                y_tiles[0] = y_t
+                y_open.append(y_t)
             nc.vector.tensor_tensor(
-                out=y_tiles[0][:, half * KPASS : (half + 1) * KPASS],
+                out=y_open[0][:, half * KPASS : (half + 1) * KPASS],
                 in0=y_ps[:],
-                in1=b_out_all[:, n * KPASS : (n + 1) * KPASS],
+                in1=b_out_all[:, col * KPASS : (col + 1) * KPASS],
                 op=ALU.add,
             )
             if half == 1:
-                nc.sync.dma_start(out=out[b, row0 : row0 + P, (n - 1) * KPASS : (n + 1) * KPASS], in_=y_tiles[0][:])
+                nc.sync.dma_start(
+                    out=out[b, row0 : row0 + P, (col - 1) * KPASS : (col + 1) * KPASS], in_=y_open.pop(0)[:]
+                )
 
         g_ready = []
 
-        def share(steps, pos, npos):
-            for r in range(steps * pos // npos, steps * (pos + 1) // npos):
+        def share(count, pos, npos):
+            for r in range(count * pos // npos, count * (pos + 1) // npos):
                 chunk_step()
 
-        def step(n):
-            steps = chunks_of_step.get(n, 0)
+        def step(st):
+            left = chunks_of_step.get(st, 0)
             todo = g_ready.pop(0) if g_ready else None
-            if steps > 0:
+            if left > 0:
                 chunk_step()
-                steps = steps - 1
+                left = left - 1
             if todo is not None:
                 make_g(todo[0], todo[1])
             for j in range(PACK):
-                if n < NSTEP:
-                    stage1_tile(n // NPASS, (n % NPASS) * PACK + j)
-                if n >= DELAY:
-                    stage2_bank((n - DELAY) // SUB, (n - DELAY) % SUB, j)
-                share(steps, j, PACK)
+                if st < NSTEP:
+                    stage1_tile(st // NPASS, (st % NPASS) * PACK + j)
+                if st >= DELAY:
+                    stage2_bank((st - DELAY) // SUB, (st - DELAY) % SUB, j)
+                share(left, j, PACK)
                 if j == 1 and todo is not None:
                     quantise_g(todo[0], todo[1])
-            if n == 2:
+            if st == 2:
                 nc.sync.dma_start(out=b_out_all[:], in_=b_out.partition_broadcast(P))
-            if n % NPASS == 1 and n // NPASS + 1 < NBLK and n > 1:
-                load_w(n // NPASS + 1)
-            if n % NPASS == 0 and NPASS <= n <= NSTEP:
-                norm(n // NPASS - 1)
-            if n % NPASS == 1 and NPASS <= n <= NSTEP + 1:
-                i = n // NPASS - 1
+            if st % NPASS == 1 and st // NPASS + 1 < NBLK and st > 1:
+                load_w(st // NPASS + 1)
+            if st % NPASS == 0 and NPASS <= st <= NSTEP:
+                norm(st // NPASS - 1)
+            if st % NPASS == 1 and NPASS <= st <= NSTEP + 1:
+                i = st // NPASS - 1
                 spread_s(i)
                 for grp in range(NPASS):
                     g_ready.append((i, grp))
@@ -425,5 +430,5 @@ def tile_hydraattention_pb_l_kernel(tc, x, mask, W_q, b_q, kv_know, kv_mask, W_o
         load_w(0)
         share(chunks_of_step[-1], 2, 3)
         load_w(1)
-        for n in range(NSTEP + DELAY):
-            step(n)
+        for st in range(NSTEP + DELAY):
+            step(st)

from contextlib import ExitStack

import concourse.mybir as mybir
from concourse.masks import make_identity

F32 = mybir.dt.float32
BF16 = mybir.dt.bfloat16
U32 = mybir.dt.uint32
U8 = mybir.dt.uint8
FP8X4 = mybir.dt.float8_e4m3fn_x4
ACT = mybir.ActivationFunctionType
ALU = mybir.AluOpType

IMAGES = 2
C = 2048
PIX = 4096
P = 128
PACK = 4
KPASS = P * PACK
NPASS = C // KPASS
T = 512
SUB = T // P
NBLK = IMAGES * PIX // T
BLK_PER_IMG = PIX // T
NCT = C // P
NSTEP = NBLK * NPASS

FLOPS = 2 * 2 * IMAGES * PIX * C * C

DELAY = 10
W_OUT_CHUNKS = (1, 1, 2, 2, 2, 2, 3, 3)

RAW_BUFS = 4
IL_BUFS = 4
U_BUFS = 3
SQ_BUFS = 3
QU_BUFS = 6
Y_BUFS = 3
S1_BANKS = 3
S2_BANKS = 3


def tile_hydraattention_pb_l_kernel(tc, x, mask, W_q, b_q, kv_know, kv_mask, W_out, b_out, out):
    nc = tc.nc
    xv = x.rearrange("b c h w -> b c (h w)")
    park = out[IMAGES - 1, PIX - IMAGES * PIX // C : PIX, :]
    mask_rows = mask.rearrange("b o h w -> (b o h w)").rearrange("(c p) -> c p", p=P)

    with ExitStack() as ctx:
        sb = ctx.enter_context(tc.tile_pool(name="sb", bufs=1))
        ps = ctx.enter_context(tc.psum_pool(name="ps", bufs=1))
        ctx.enter_context(tc.manual_schedule())

        wq_codes = sb.tile([P, NPASS, C], U32, name="wqc", align_bytes=64)
        wq_scales = sb.tile([P, C], U8, name="wqs", align_bytes=64)
        wo_codes = sb.tile([P, NPASS, C], U32, name="woc", align_bytes=64)
        wo_scales = sb.tile([P, C], U8, name="wos", align_bytes=64)

        chunks = []
        done = {"load": 0, "copy": 0, "quant": 0}
        last_chunk = {}
        raws = {}
        interleaved = {}
        x_codes = {}
        x_scales = {}

        def x_target(i, g):
            def target():
                if i not in x_codes:
                    xc_t = sb.tile([P, NPASS, T], U32, tag="xc", bufs=2, align_bytes=64, name="xc")
                    xs_t = sb.tile([P, T], U8, tag="xs", bufs=2, align_bytes=64, name="xs")
                    x_codes[i] = xc_t
                    x_scales[i] = xs_t
                return x_codes[i][:, g, :], x_scales[i][4 * g : P, :]

            return target

        def w_target(codes, scales, g, c0):
            def target():
                return codes[:, g, c0 : c0 + KPASS], scales[4 * g : P, c0 : c0 + KPASS]

            return target

        def load_ahead():
            while done["load"] < len(chunks) and done["load"] < done["copy"] + RAW_BUFS:
                ci = done["load"]
                raw = sb.tile([P, PACK, KPASS], BF16, tag="raw", bufs=RAW_BUFS, name="raw")
                nc.sync.dma_start(out=raw[:], in_=chunks[ci][0].rearrange("(p j) w -> p j w", j=PACK))
                raws[ci] = raw
                done["load"] = ci + 1

        def copy_next():
            ci = done["copy"]
            raw = raws.pop(ci)
            il = sb.tile([P, PACK * KPASS], BF16, tag="il", bufs=IL_BUFS, align_bytes=64, name="il")
            if chunks[ci][1]:
                dst = il[:].rearrange("p (t m j) -> p m j t", t=PACK, j=PACK)
                src = raw[:].rearrange("p j (m t) -> p m j t", t=PACK)
            else:
                dst = il[:].rearrange("p (c i j) -> p c j i", i=PACK, j=PACK)
                src = raw[:].rearrange("p j (c i) -> p c j i", i=PACK)
            if chunks[ci][2] == "vector":
                nc.vector.tensor_copy(out=dst, in_=src)
            else:
                nc.scalar.copy(out=dst, in_=src)
            interleaved[ci] = il
            done["copy"] = ci + 1
            load_ahead()

        def quantise_next():
            ci = done["quant"]
            il = interleaved.pop(ci)
            codes, scales = chunks[ci][3]()
            nc.vector.quantize_mx(out=codes.bitcast(FP8X4), scales=scales, in_=il[:])
            done["quant"] = ci + 1

        def need(key):
            while done["quant"] <= last_chunk[key]:
                if done["copy"] <= done["quant"]:
                    copy_next()
                quantise_next()

        def chunk_step():
            copy_next()
            while done["quant"] < done["copy"] - 1:
                quantise_next()

        x_list = [(i, g) for i in range(NBLK) for g in range(NPASS)]
        wq_list = [(grp, g) for grp in range(NPASS) for g in range(NPASS)]
        wo_list = [(col, g) for col in range(NPASS) for g in range(NPASS)]

        def add_x(engine):
            i, g = x_list.pop(0)
            b = i // BLK_PER_IMG
            t0 = (i % BLK_PER_IMG) * T
            chunks.append((xv[b, g * KPASS : (g + 1) * KPASS, t0 : t0 + T], False, engine, x_target(i, g)))
            last_chunk[("x", i)] = len(chunks) - 1

        def add_wq():
            grp, g = wq_list.pop(0)
            rows = W_q[g * KPASS : (g + 1) * KPASS, grp * KPASS : (grp + 1) * KPASS]
            engine = "scalar" if g % 2 == 0 else "vector"
            chunks.append((rows, True, engine, w_target(wq_codes, wq_scales, g, grp * KPASS)))
            last_chunk[("wq", grp)] = len(chunks) - 1

        def add_wo():
            col, g = wo_list.pop(0)
            rows = W_out[g * KPASS : (g + 1) * KPASS, col * KPASS : (col + 1) * KPASS]
            chunks.append((rows, False, "scalar", w_target(wo_codes, wo_scales, g, col * KPASS)))
            last_chunk[("wo", col)] = len(chunks) - 1

        chunks_of_step = {}
        for st in range(-1, NSTEP):
            before = len(chunks)
            if st == -1:
                for r in range(NPASS):
                    add_x("vector")
                for r in range(2 * NPASS):
                    add_wq()
            elif st < DELAY:
                if st == 0:
                    add_x("vector")
                if st < 2:
                    for r in range(NPASS):
                        add_wq()
                else:
                    for r in range(W_OUT_CHUNKS[st - 2]):
                        add_wo()
                add_x("vector")
            elif x_list:
                add_x("scalar")
            chunks_of_step[st] = len(chunks) - before

        load_ahead()

        mrow = sb.tile([P, P], BF16, name="mrow")
        nc.vector.memset(mrow[:], 0.0)
        nc.scalar.dma_start(out=mrow[0:64, :], in_=mask_rows)
        bq_r = sb.tile([P, NPASS, PACK], BF16, name="bq_r")
        nc.scalar.dma_start(out=bq_r[:], in_=b_q.rearrange("(g p j) -> p g j", p=P, j=PACK))
        kk_r = sb.tile([P, IMAGES * NPASS, PACK], BF16, name="kk_r")
        nc.scalar.dma_start(out=kk_r[:], in_=kv_know.rearrange("b o (g p j) -> p (b o g) j", p=P, j=PACK))
        km_r = sb.tile([P, IMAGES * NPASS, PACK], BF16, name="km_r")
        nc.scalar.dma_start(out=km_r[:], in_=kv_mask.rearrange("b o (g p j) -> p (b o g) j", p=P, j=PACK))
        b_out_all = sb.tile([P, C], BF16, name="bob")

        warm = sb.tile([P, 1], F32, name="warm")
        nc.vector.memset(warm[:], 1.0)
        warm2 = sb.tile([P, 1], F32, name="warm2")
        nc.scalar.activation(out=warm2[:], in_=warm[:], func=ACT.Sqrt)

        ones2 = sb.tile([P, 2], F32, name="ones2")
        nc.vector.memset(ones2[:], 1.0)
        ident_bf = sb.tile([P, P], BF16, name="identb")
        make_identity(nc, ident_bf[:])
        ident_f32 = sb.tile([P, P], F32, name="identf")
        make_identity(nc, ident_f32[:])

        def constants():
            bq = sb.tile([P, NCT], F32, name="bq")
            nc.vector.tensor_copy(out=bq[:], in_=bq_r[:].rearrange("p g j -> p (g j)"))
            kvk = sb.tile([P, IMAGES * NCT], F32, name="kvk")
            nc.vector.tensor_copy(out=kvk[:], in_=kk_r[:].rearrange("p g j -> p (g j)"))
            dk = sb.tile([P, IMAGES * NCT], F32, name="dk")
            nc.vector.tensor_tensor(
                out=dk[:],
                in0=km_r[:].rearrange("p g j -> p (g j)"),
                in1=kk_r[:].rearrange("p g j -> p (g j)"),
                op=ALU.subtract,
            )
            mc = sb.tile([P, P], F32, name="mc")
            nc.vector.tensor_copy(out=mc[:], in_=mrow[:])
            inv = sb.tile([P, P], F32, name="inv")
            nc.vector.tensor_scalar(out=inv[:], in0=mc[:], scalar1=-1.0, scalar2=1.0, op0=ALU.mult, op1=ALU.add)
            e07 = sb.tile([P, P], F32, name="e07")
            nc.vector.tensor_scalar(out=e07[:], in0=mc[:], scalar1=-0.7, scalar2=1.0, op0=ALU.mult, op1=ALU.add)
            ca = sb.tile([P, P], F32, name="ca")
            nc.vector.tensor_tensor(out=ca[:], in0=inv[:], in1=e07[:], op=ALU.mult)
            cb = sb.tile([P, P], F32, name="cb")
            nc.vector.scalar_tensor_tensor(out=cb[:], in0=mc[:], scalar=0.7, in1=mc[:], op0=ALU.mult, op1=ALU.mult)
            sig_r = sb.tile([P, P], F32, name="sig_r")
            nc.vector.tensor_tensor(out=sig_r[:], in0=ca[:], in1=cb[:], op=ALU.add)
            rsig = sb.tile([P, P], F32, name="rsig")
            nc.vector.reciprocal(out=rsig[:], in_=sig_r[:])
            w_r = sb.tile([P, P], F32, name="w_r")
            nc.vector.tensor_tensor(out=w_r[:], in0=cb[:], in1=rsig[:], op=ALU.mult)
            nrows = IMAGES * PIX // P
            nc.sync.dma_start(out=park.rearrange("r (c p) -> (r c) p", p=P), in_=w_r[0:nrows, :])
            sig_ps = ps.tile([P, P], F32, tag="misc", bufs=1, name="s_ps")
            nc.tensor.transpose(out=sig_ps[:], in_=sig_r[:], identity=ident_f32[:])
            sigma = sb.tile([P, nrows], F32, name="sig")
            nc.vector.tensor_copy(out=sigma[:], in_=sig_ps[:, 0:nrows])
            return bq, kvk, dk, sigma

        w_all = {}
        u_tiles = {}
        qu_tiles = {}
        sums = {}
        s_parts = {}
        s_all = {}
        g_tiles = {}
        g_codes = {}
        g_scales = {}
        y_open = []

        def load_w(i):
            wb = sb.tile([P, T], F32, tag="wb", bufs=2, name="wb")
            per_row = C // T
            src = park[i // per_row, (i % per_row) * T : (i % per_row + 1) * T]
            nc.sync.dma_start(out=wb[:], in_=src.partition_broadcast(P))
            w_all[i] = wb

        def make_u(tile_no):
            if tile_no in u_tiles or tile_no >= NBLK * NCT:
                return
            i = tile_no // NCT
            v = (i // BLK_PER_IMG) * NCT + tile_no % NCT
            u = sb.tile([P, T], F32, tag="u", bufs=U_BUFS, name="u")
            nc.scalar.activation(
                out=u[:], in_=w_all[i][:], func=ACT.Identity, bias=kvk[:, v : v + 1], scale=dk[:, v : v + 1]
            )
            u_tiles[tile_no] = u

        def stage1_tile(i, ct):
            tile_no = i * NCT + ct
            grp = ct // PACK
            j = ct % PACK
            need(("x", i))
            need(("wq", grp))
            make_u(tile_no)
            q_ps = ps.tile([P, T], F32, tag="s1", bufs=S1_BANKS, name="s1")
            for g in range(NPASS):
                nc.tensor.matmul_mx(
                    out=q_ps[:],
                    lhsT=wq_codes[:, g, ct * P : (ct + 1) * P].bitcast(FP8X4),
                    lhsT_scale=wq_scales[4 * g : P, ct * P : (ct + 1) * P],
                    rhs=x_codes[i][:, g, :].bitcast(FP8X4),
                    rhs_scale=x_scales[i][4 * g : P, :],
                    start=(g == 0),
                    stop=(g == NPASS - 1),
                )
            make_u(tile_no + 1)
            opens_sum = i not in sums
            if opens_sum:
                sq = sb.tile([P, T], F32, tag="accg", bufs=2, name="accg")
                sums[i] = sq
            else:
                sq = sb.tile([P, T], F32, tag="sq", bufs=SQ_BUFS, name="sq")
            nc.scalar.activation(out=sq[:], in_=q_ps[:], func=ACT.Square, bias=bq[:, ct : ct + 1], scale=1.0)
            if j == 0:
                qu_t = sb.tile([P, PACK, T], F32, tag="qu", bufs=QU_BUFS, name="qu")
                qu_tiles[(i, grp)] = qu_t
            nc.vector.scalar_tensor_tensor(
                out=qu_tiles[(i, grp)][:, j, :],
                in0=q_ps[:],
                scalar=bq[:, ct : ct + 1],
                in1=u_tiles.pop(tile_no)[:],
                op0=ALU.add,
                op1=ALU.mult,
            )
            if not opens_sum:
                nc.gpsimd.tensor_tensor(out=sums[i][:], in0=sums[i][:], in1=sq[:], op=ALU.add)

        def norm(i):
            n_ps = ps.tile([P, 2 * SUB], F32, tag="misc", bufs=1, name="nps")
            total = sums.pop(i)
            for tt in range(SUB):
                nc.tensor.matmul(
                    out=n_ps[:, 2 * tt : 2 * tt + 2],
                    lhsT=total[:, tt * P : (tt + 1) * P],
                    rhs=ones2[:],
                    start=True,
                    stop=True,
                )
            nrm = sb.tile([P, SUB], F32, tag="nrm", bufs=2, name="nrm")
            nc.scalar.activation(out=nrm[:], in_=n_ps[:].rearrange("p (k two) -> p k two", two=2)[:, :, 0], func=ACT.Sqrt)
            rn = sb.tile([P, SUB], F32, tag="rn", bufs=2, name="rn")
            nc.vector.reciprocal(out=rn[:], in_=nrm[:])
            sc = sb.tile([P, SUB], F32, tag="sc", bufs=2, name="sc")
            nc.vector.tensor_tensor(out=sc[:], in0=rn[:], in1=sigma[:, i * SUB : (i + 1) * SUB], op=ALU.mult)
            s_hi = sb.tile([P, SUB], BF16, tag="s_hi", bufs=2, name="s_hi")
            nc.vector.tensor_copy(out=s_hi[:], in_=sc[:])
            s_lo = sb.tile([P, SUB], BF16, tag="s_lo", bufs=2, name="s_lo")
            nc.vector.tensor_tensor(out=s_lo[:], in0=sc[:], in1=s_hi[:], op=ALU.subtract)
            s_parts[i] = (s_hi, s_lo)

        def spread_s(i):
            parts = s_parts.pop(i)
            s_ps = ps.tile([P, T], F32, tag="sps", bufs=1, name="sps")
            for tt in range(SUB):
                for r in range(2):
                    nc.tensor.matmul(
                        out=s_ps[:, tt * P : (tt + 1) * P],
                        lhsT=parts[r][:, tt : tt + 1].to_broadcast([P, P]),
                        rhs=ident_bf[:],
                        start=(r == 0),
                        stop=(r == 1),
                    )
            s_all[i] = s_ps

        def make_g(i, grp):
            gi = sb.tile([P, T, PACK], BF16, tag="gi", bufs=2, align_bytes=64, name="gi")
            nc.vector.tensor_tensor(
                out=gi[:].rearrange("p (c i) j -> p c j i", i=PACK),
                in0=qu_tiles.pop((i, grp))[:].rearrange("p j (c i) -> p c j i", i=PACK),
                in1=s_all[i][:].rearrange("p (c i) -> p c i", i=PACK).unsqueeze(2).to_broadcast([P, T // PACK, PACK, PACK]),
                op=ALU.mult,
            )
            g_tiles[(i, grp)] = gi

        def quantise_g(i, grp):
            if i not in g_codes:
                gc_t = sb.tile([P, NPASS, T], U32, tag="gc", bufs=2, align_bytes=64, name="gc")
                gs_t = sb.tile([P, T], U8, tag="gs", bufs=2, align_bytes=64, name="gs")
                g_codes[i] = gc_t
                g_scales[i] = gs_t
            nc.vector.quantize_mx(
                out=g_codes[i][:, grp, :].bitcast(FP8X4),
                scales=g_scales[i][4 * grp : P, :],
                in_=g_tiles.pop((i, grp))[:].rearrange("p t j -> p (t j)"),
            )

        def stage2_bank(i, tt, col):
            b = i // BLK_PER_IMG
            row0 = (i % BLK_PER_IMG) * T + tt * P
            need(("wo", col))
            y_ps = ps.tile([P, KPASS], F32, tag="s2", bufs=S2_BANKS, name="s2")
            for g in range(NPASS):
                nc.tensor.matmul_mx(
                    out=y_ps[:],
                    lhsT=g_codes[i][:, g, tt * P : (tt + 1) * P].bitcast(FP8X4),
                    lhsT_scale=g_scales[i][4 * g : P, tt * P : (tt + 1) * P],
                    rhs=wo_codes[:, g, col * KPASS : (col + 1) * KPASS].bitcast(FP8X4),
                    rhs_scale=wo_scales[4 * g : P, col * KPASS : (col + 1) * KPASS],
                    start=(g == 0),
                    stop=(g == NPASS - 1),
                )
            half = col % 2
            if half == 0:
                y_t = sb.tile([P, 2 * KPASS], F32, tag="y", bufs=Y_BUFS, name="y")
                y_open.append(y_t)
            nc.vector.tensor_tensor(
                out=y_open[0][:, half * KPASS : (half + 1) * KPASS],
                in0=y_ps[:],
                in1=b_out_all[:, col * KPASS : (col + 1) * KPASS],
                op=ALU.add,
            )
            if half == 1:
                nc.sync.dma_start(
                    out=out[b, row0 : row0 + P, (col - 1) * KPASS : (col + 1) * KPASS], in_=y_open.pop(0)[:]
                )

        g_ready = []

        def share(count, pos, npos):
            for r in range(count * pos // npos, count * (pos + 1) // npos):
                chunk_step()

        def step(st):
            left = chunks_of_step.get(st, 0)
            todo = g_ready.pop(0) if g_ready else None
            if left > 0:
                chunk_step()
                left = left - 1
            if todo is not None:
                make_g(todo[0], todo[1])
            for j in range(PACK):
                if st < NSTEP:
                    stage1_tile(st // NPASS, (st % NPASS) * PACK + j)
                if st >= DELAY:
                    stage2_bank((st - DELAY) // SUB, (st - DELAY) % SUB, j)
                share(left, j, PACK)
                if j == 1 and todo is not None:
                    quantise_g(todo[0], todo[1])
            if st == 2:
                nc.sync.dma_start(out=b_out_all[:], in_=b_out.partition_broadcast(P))
            if st % NPASS == 1 and st // NPASS + 1 < NBLK and st > 1:
                load_w(st // NPASS + 1)
            if st % NPASS == 0 and NPASS <= st <= NSTEP:
                norm(st // NPASS - 1)
            if st % NPASS == 1 and NPASS <= st <= NSTEP + 1:
                i = st // NPASS - 1
                spread_s(i)
                for grp in range(NPASS):
                    g_ready.append((i, grp))

        share(chunks_of_step[-1], 0, 3)
        bq, kvk, dk, sigma = constants()
        share(chunks_of_step[-1], 1, 3)
        load_w(0)
        share(chunks_of_step[-1], 2, 3)
        load_w(1)
        for st in range(NSTEP + DELAY):
            step(st)
